import numpy as np
import ml_dtypes


def mxq(x, axis, fmt="e4m3"):
    dtype, down = {"e4m3": (ml_dtypes.float8_e4m3fn, 7), "e5m2": (ml_dtypes.float8_e5m2, 14)}[fmt]
    v = np.moveaxis(np.asarray(x, np.float32).astype(ml_dtypes.bfloat16).astype(np.float64), axis, -1)
    blocks = v.reshape(v.shape[:-1] + (-1, 32))
    amax = np.abs(blocks).max(-1, keepdims=True)
    byte = np.maximum(np.where(amax > 0, np.frexp(amax)[1] - 1 + 127, 0) - down, 1)
    scale = np.exp2(byte - 127.0)
    codes = (blocks / scale).astype(np.float32).astype(dtype).astype(np.float64)
    return np.moveaxis((codes * scale).reshape(v.shape), -1, axis)


WIDE = False


def mx_kscale(k):
    if not WIDE:
        return np.ones(k)
    levels = np.array([10, -10, 5, -5, 0])
    if k % 512:
        return np.exp2(np.random.permutation(np.resize(levels, k // 32))).repeat(32)
    a = np.empty((k // 512, 16))
    for p in range(k // 512):
        a[p, :8] = np.random.permutation(np.resize(levels, 8))
        for g in range(8):
            far = levels[np.abs(levels - a[p, g]) >= 10]
            a[p, g + 8] = far[np.random.randint(len(far))]
    return np.exp2(a.ravel()).repeat(32)


BF16 = ml_dtypes.bfloat16


def bf(x):
    return np.asarray(x, np.float32).astype(BF16)


def f64(x):
    return np.asarray(x).astype(np.float64)


B, T, M, H, D, C = 1, 1024, 2048, 8, 128, 512
ROTARY_BASE = 10000.0
HALF = D // 2


def rope(u):
    pos = np.arange(T, dtype=np.float64)
    dims = np.arange(HALF, dtype=np.float64)
    ang_freqs = ROTARY_BASE ** (-dims / HALF)
    radians = pos[:, None] * ang_freqs[None, :]
    cos = np.cos(radians)[None, :, None, :]
    sin = np.sin(radians)[None, :, None, :]
    even, odd = u[..., :HALF], u[..., HALF:]
    return np.concatenate([even * cos - odd * sin, even * sin + odd * cos], axis=-1)


def draw0():
    s = mx_kscale(M)
    return {"x": bf(np.random.standard_normal((B, T, M)) * s),
            "w_aq": bf(np.random.standard_normal((H, M, D)) * 2.0 / np.sqrt(M) / s[None, :, None]),
            "w_ak": bf(np.random.standard_normal((H, M, D)) * 2.0 / np.sqrt(M) / s[None, :, None])}


def core(x, w_aq, w_ak):
    xq = mxq(f64(x), 2, "e4m3")[:, None, :, :]
    q = (xq @ mxq(f64(w_aq), 1, "e4m3")[None]).transpose(0, 2, 1, 3)
    k = (xq @ mxq(f64(w_ak), 1, "e4m3")[None]).transpose(0, 2, 1, 3)
    return rope(q), rope(k)


def e4m3fn_bytes(y):
    return np.clip(np.asarray(y, np.float64), -448.0, 448.0).astype(np.float32).astype(ml_dtypes.float8_e4m3fn).view(np.uint8)


def e4m3fn_values(b):
    return np.asarray(b, np.uint8).view(ml_dtypes.float8_e4m3fn).astype(np.float64)


def setup_inputs():
    d = draw0()
    x0 = np.asarray(d['x']).astype(np.float64)
    s = (np.max(np.abs(x0), axis=(0, 1), keepdims=True) / 448.0).astype(np.float32)
    out = {}
    for k, v in d.items():
        if k == 'x':
            out['x_bytes'] = e4m3fn_bytes(x0 / s.astype(np.float64))
            out['x_scale'] = s
        else:
            out[k] = v
    return out


def reference(x_bytes, x_scale, w_aq, w_ak):
    return core(e4m3fn_values(x_bytes) * x_scale.astype(np.float64), w_aq, w_ak)

@@ -1,0 +1,269 @@
+from contextlib import ExitStack
+
+import concourse.mybir as mybir
+from concourse.masks import make_identity
+
+F32 = mybir.dt.float32
+BF16 = mybir.dt.bfloat16
+I32 = mybir.dt.int32
+U32 = mybir.dt.uint32
+U8 = mybir.dt.uint8
+FP8 = mybir.dt.float8_e4m3fn
+FP8X4 = mybir.dt.float8_e4m3fn_x4
+ALU = mybir.AluOpType
+ACT = mybir.ActivationFunctionType
+
+P = 128
+TOK = 1024
+KDIM = 2048
+HEADS = 8
+HD = 128
+HALF = 64
+NT = TOK // P
+NG = KDIM // 512
+NQ = 4
+FLOPS = 2 * TOK * KDIM * 2 * HEADS * HD
+
+PI = 3.141592653589793
+TWO_PI = 2.0 * PI
+C1 = round(TWO_PI * 8192.0) / 8192.0
+C2 = TWO_PI - C1
+ROTARY_BASE = 10000.0
+
+
+def tile_multiheadselfattention_pa_kernel(tc, x_bytes, x_scale, w_aq, w_ak, out_0, out_1):
+    nc = tc.nc
+    xrows = x_bytes.flatten_outer_dims()
+    outs = [out_0.rearrange("b t h d -> (b t) (h d)"), out_1.rearrange("b t h d -> (b t) (h d)")]
+    ws_in = [w_aq, w_ak]
+    NC = NQ * NG
+
+    with ExitStack() as ctx:
+        keep = ctx.enter_context(tc.tile_pool(name="keep", bufs=1))
+        tmp = ctx.enter_context(tc.tile_pool(name="tmp", bufs=1))
+        wrp = ctx.enter_context(tc.tile_pool(name="wrp", bufs=8))
+        xbp = ctx.enter_context(tc.tile_pool(name="xbp", bufs=3))
+        xgp = ctx.enter_context(tc.tile_pool(name="xgp", bufs=2))
+        wgp = ctx.enter_context(tc.tile_pool(name="wgp", bufs=3))
+        abp = ctx.enter_context(tc.tile_pool(name="abp", bufs=4))
+        psum = ctx.enter_context(tc.psum_pool(name="psum", bufs=8))
+        ctx.enter_context(tc.manual_schedule())
+
+        sc = keep.tile([P, KDIM], F32, name="sc")
+        xby = keep.tile([P, NT * KDIM], U8, name="xby")
+        ident = keep.tile([P, P], F32, name="ident")
+        tab = keep.tile([P, NT, 2, 2, HALF], F32, name="tab")
+        xc = keep.tile([P, NT * NG * P], U32, name="xc", align_bytes=64)
+        xs = keep.tile([P, NT * NG * P], U8, name="xs", align_bytes=64)
+        wc = keep.tile([P, NC * 512], U32, name="wc", align_bytes=64)
+        wsc = keep.tile([P, NC * 512], U8, name="wsc", align_bytes=64)
+        wraw_t = {}
+
+        nc.scalar.dma_start(out=sc[:], in_=x_scale.rearrange("a b k -> (a b k)").partition_broadcast(P))
+
+        def load_x(t):
+            nc.sync.dma_start(out=xby[:, t * KDIM:(t + 1) * KDIM], in_=xrows[t * P:(t + 1) * P, :])
+
+        def load_w(c):
+            q, g = divmod(c, NG)
+            w = ws_in[q // 2]
+            h0 = 4 * (q % 2)
+            wraw = wrp.tile([P, 4, 512], BF16, name="wraw")
+            wraw_t[c] = wraw
+            nc.sync.dma_start(
+                out=wraw[:],
+                in_=w[h0:h0 + 4, g * 512:(g + 1) * 512, :].rearrange("h (p j) d -> p h (j d)", j=4),
+            )
+
+        load_x(0)
+        load_x(1)
+        for t in range(2, NT):
+            load_w(t - 2)
+            load_x(t)
+        load_w(6)
+        load_w(7)
+
+        zero = tmp.tile([P, 1], F32, name="zero")
+        warm = tmp.tile([P, 1], F32, name="warm")
+        nc.vector.memset(zero[:], 0.0)
+        nc.scalar.activation(out=warm[:], in_=zero[:], func=ACT.Sin)
+
+        ang = tmp.tile([P, NT * HALF], F32, name="ang")
+        ni = tmp.tile([P, NT * HALF], I32, name="ni")
+        nf = tmp.tile([P, NT * HALF], F32, name="nf")
+        ra = tmp.tile([P, NT * HALF], F32, name="ra")
+        sh = tmp.tile([P, NT, HALF], F32, name="sh")
+        ch = tmp.tile([P, NT, HALF], F32, name="ch")
+        sq = tmp.tile([P, NT, HALF], F32, name="sq")
+        nc.gpsimd.iota(ang[:], pattern=[[P, NT], [0, HALF]], base=0, channel_multiplier=1,
+                       allow_small_or_imprecise_dtypes=True)
+        make_identity(nc, ident[:])
+        W2 = NT * HALF // 2
+        halves = [slice(0, W2), slice(W2, 2 * W2)]
+        for b in range(6):
+            low = 1 << b
+            for hs in halves:
+                v = ang[:, hs].rearrange("p (a two l) -> p a two l", two=2, l=low)[:, :, 1, :]
+                nc.vector.tensor_scalar(out=v, in0=v, scalar1=ROTARY_BASE ** (-low / 64.0), scalar2=None, op0=ALU.mult)
+        for hs in halves:
+            nc.vector.tensor_scalar(out=ni[:, hs], in0=ang[:, hs], scalar1=1.0 / TWO_PI, scalar2=None, op0=ALU.mult)
+        for hs in halves:
+            nc.vector.tensor_copy(out=nf[:, hs], in_=ni[:, hs])
+        for hs in halves:
+            nc.vector.scalar_tensor_tensor(out=ang[:, hs], in0=nf[:, hs], scalar=-C1, in1=ang[:, hs], op0=ALU.mult, op1=ALU.add)
+        for hs in halves:
+            nc.vector.scalar_tensor_tensor(out=ang[:, hs], in0=nf[:, hs], scalar=-C2, in1=ang[:, hs], op0=ALU.mult, op1=ALU.add)
+        for hs in halves:
+            nc.vector.scalar_tensor_tensor(out=ra[:, hs], in0=ang[:, hs], scalar=-1.0, in1=ang[:, hs], op0=ALU.mult, op1=ALU.max)
+        nc.scalar.activation(out=sh[:].rearrange("p t i -> p (t i)"), in_=ang[:], func=ACT.Sin, scale=0.5)
+        nc.scalar.activation(out=ch[:].rearrange("p t i -> p (t i)"), in_=ra[:], func=ACT.Sin, scale=-0.5, bias=0.5 * PI)
+
+        def tables_finish():
+            nc.vector.scalar_tensor_tensor(out=tab[:, :, 1, 0, :], in0=sh[:], scalar=2.0, in1=ch[:], op0=ALU.mult, op1=ALU.mult)
+            nc.vector.tensor_tensor(out=sq[:], in0=sh[:], in1=sh[:], op=ALU.mult)
+            nc.scalar.activation(out=tab[:, :, 1, 1, :], in_=tab[:, :, 1, 0, :], func=ACT.Copy, scale=-1.0)
+            nc.scalar.activation(out=tab[:, :, 0, :, :], in_=sq[:].unsqueeze(2).to_broadcast([P, NT, 2, HALF]),
+                                 func=ACT.Copy, scale=-2.0, bias=1.0)
+
+        xb_t = {}
+        xg_t = {}
+        xt_t = {}
+        ps_t = {}
+        ab_t = {}
+        wg_t = {}
+
+        def x_product(t, pieces):
+            xb = xbp.tile([P, KDIM], BF16, name="xb")
+            w = KDIM // pieces
+            for c in range(pieces):
+                nc.vector.tensor_tensor(out=xb[:, c * w:(c + 1) * w],
+                                        in0=xby[:, t * KDIM + c * w:t * KDIM + (c + 1) * w].bitcast(FP8),
+                                        in1=sc[:, c * w:(c + 1) * w], op=ALU.mult)
+            xb_t[t] = xb
+
+        def x_turn(t):
+            words = xb_t[t][:].bitcast(F32)
+            banks = []
+            for b in range(2):
+                xt = psum.tile([P, 512], F32, name="xt", tag="bank")
+                banks.append(xt)
+                for gl in range(2):
+                    g = 2 * b + gl
+                    for u in range(2):
+                        nc.tensor.transpose(xt[:, (2 * gl + u) * P:(2 * gl + u + 1) * P],
+                                            words[:, 256 * g + u:256 * (g + 1):2], ident[:])
+            xt_t[t] = banks
+
+        def x_copy(t):
+            if t % 2 == 0:
+                xg = xgp.tile([P, 2 * KDIM], BF16, name="xg", align_bytes=64)
+                xg_t[t // 2] = xg
+            xg = xg_t[t // 2]
+            j = t % 2
+            xgw = xg[:, j * KDIM:(j + 1) * KDIM].bitcast(F32).rearrange("p (g r u) -> p g r u", g=NG, u=2)
+            for b in range(2):
+                nc.scalar.copy(out=xgw[:, 2 * b:2 * b + 2], in_=xt_t[t][b][:].rearrange("p (g u r) -> p g r u", g=2, u=2))
+
+        def x_quant(k):
+            lo = k * 2 * NG * P
+            hi = lo + 2 * NG * P
+            nc.vector.quantize_mx(out=xc[:, lo:hi].bitcast(FP8X4), scales=xs[:, lo:hi], in_=xg_t[k][:])
+
+        def w_group(c):
+            if c % 2 == 0:
+                wg = wgp.tile([P, 2, 512, 4], BF16, name="wg", align_bytes=64)
+                wg_t[c // 2] = wg
+            wg = wg_t[c // 2]
+            nc.scalar.copy(out=wg[:, c % 2].rearrange("p (h d) j -> p h d j", h=4),
+                           in_=wraw_t[c][:].rearrange("p h (j d) -> p h d j", j=4))
+
+        def w_quant(k):
+            lo = k * 1024
+            nc.vector.quantize_mx(out=wc[:, lo:lo + 1024].bitcast(FP8X4), scales=wsc[:, lo:lo + 1024],
+                                  in_=wg_t[k][:].rearrange("p e c j -> p (e c j)"))
+
+        def products(i):
+            q, t = divmod(i, NT)
+            ps = psum.tile([P, 512], F32, name="ps", tag="bank")
+            ps_t[i] = ps
+            for g in range(NG):
+                xo = (t * NG + g) * P
+                wo = (q * NG + g) * 512
+                nc.tensor.matmul_mx(out=ps[:], lhsT=xc[:, xo:xo + P].bitcast(FP8X4), lhsT_scale=xs[:, xo:xo + P],
+                                    rhs=wc[:, wo:wo + 512].bitcast(FP8X4), rhs_scale=wsc[:, wo:wo + 512],
+                                    start=(g == 0), stop=(g == NG - 1))
+
+        def rotate(i):
+            t = i % NT
+            if i % 2 == 0:
+                ab = abp.tile([P, 2, 2, 4, HD], F32, name="ab")
+                ab_t[i // 2] = ab
+            nc.vector.tensor_tensor(
+                out=ab_t[i // 2][:, :, i % 2],
+                in0=ps_t[i][:].rearrange("p (h d) -> p h d", h=4).unsqueeze(1).to_broadcast([P, 2, 4, HD]),
+                in1=tab[:, t].rearrange("p r f i -> p r (f i)").unsqueeze(2).to_broadcast([P, 2, 4, HD]),
+                op=ALU.mult,
+            )
+
+        def finish(k):
+            q, tp = divmod(k, NT // 2)
+            ab = ab_t[k]
+            dst = outs[q // 2][2 * tp * P:(2 * tp + 2) * P, (q % 2) * 512:(q % 2 + 1) * 512].rearrange("(j p) c -> p j c", p=P)
+            a0 = ab[:, 0].rearrange("p j h (f i) -> p (j h) f i", f=2)
+            a1 = ab[:, 1].rearrange("p j h (f i) -> p (j h) f i", f=2)[:, :, ::-1, :]
+            nc.gpsimd.tensor_tensor(out=a0, in0=a0, in1=a1, op=ALU.add)
+            nc.sync.dma_start(out=dst, in_=ab[:, 0].rearrange("p j h d -> p j (h d)"))
+
+        def finish_tile(i):
+            k, j = divmod(i, 2)
+            q, tp = divmod(k, NT // 2)
+            ab = ab_t[k]
+            dst = outs[q // 2][i % NT * P:(i % NT + 1) * P, (q % 2) * 512:(q % 2 + 1) * 512]
+            a0 = ab[:, 0, j].rearrange("p h (f i) -> p h f i", f=2)
+            a1 = ab[:, 1, j].rearrange("p h (f i) -> p h f i", f=2)[:, :, ::-1, :]
+            nc.vector.tensor_tensor(out=a0, in0=a0, in1=a1, op=ALU.add)
+            nc.sync.dma_start(out=dst, in_=ab[:, 0, j].rearrange("p h d -> p (h d)"))
+
+        AHEAD = 2
+        VTILES = NQ * NT - 4
+        LATE = 2
+        issued = 0
+        for t in range(NT):
+            x_product(t, 1)
+            x_turn(t)
+            if t < NT - LATE:
+                w_group(t)
+                load_w(t + 8)
+            x_copy(t)
+            if t == 0:
+                tables_finish()
+            if t % 2 == 1 and t >= 3:
+                w_quant(t // 2 - 1)
+                x_quant(t // 2 - 1)
+            if t in (5, 6):
+                products(issued)
+                products(issued + 1)
+                issued += 2
+
+        grouped = NT - LATE
+        for i in range(NQ * NT):
+            if i < LATE:
+                w_group(grouped)
+                load_w(grouped + 8)
+                grouped += 1
+            elif i % 2 == 0 and grouped < NC:
+                w_group(grouped)
+                grouped += 1
+            if i == 2:
+                x_quant(3)
+            elif i % 4 == 2 and i <= 22:
+                w_quant(2 + i // 4)
+            while issued < NQ * NT and issued <= i + AHEAD:
+                products(issued)
+                issued += 1
+            rotate(i)
+            if i > VTILES:
+                finish_tile(i - 1)
+            elif i % 2 == 1 and i < VTILES:
+                finish(i // 2)
+        finish_tile(NQ * NT - 1)

@@ -89,6 +89,8 @@ def tile_multiheadselfattention_pa_kernel(tc, x_bytes, x_scale, w_aq, w_ak, out_
         nc.scalar.activation(out=warm[:], in_=zero[:], func=ACT.Sin)
 
         ang = tmp.tile([P, NT * HALF], F32, name="ang")
+        fparts = tmp.tile([P, 2, 8], F32, name="fparts")
+        freq = tmp.tile([P, 8, 8], F32, name="freq")
         ni = tmp.tile([P, NT * HALF], I32, name="ni")
         nf = tmp.tile([P, NT * HALF], F32, name="nf")
         ra = tmp.tile([P, NT * HALF], F32, name="ra")
@@ -100,11 +102,18 @@ def tile_multiheadselfattention_pa_kernel(tc, x_bytes, x_scale, w_aq, w_ak, out_
         make_identity(nc, ident[:])
         W2 = NT * HALF // 2
         halves = [slice(0, W2), slice(W2, 2 * W2)]
-        for b in range(6):
+        nc.vector.memset(fparts[:], 1.0)
+        for b in range(3):
             low = 1 << b
-            for hs in halves:
-                v = ang[:, hs].rearrange("p (a two l) -> p a two l", two=2, l=low)[:, :, 1, :]
-                nc.vector.tensor_scalar(out=v, in0=v, scalar1=ROTARY_BASE ** (-low / 64.0), scalar2=None, op0=ALU.mult)
+            for part, step in ((0, 1), (1, 8)):
+                v = fparts[:, part].rearrange("p (a two l) -> p a two l", two=2, l=low)[:, :, 1, :]
+                nc.vector.tensor_scalar(out=v, in0=v, scalar1=ROTARY_BASE ** (-low * step / 64.0), scalar2=None, op0=ALU.mult)
+        nc.vector.tensor_tensor(out=freq[:], in0=fparts[:, 1].unsqueeze(2).to_broadcast([P, 8, 8]),
+                                in1=fparts[:, 0].unsqueeze(1).to_broadcast([P, 8, 8]), op=ALU.mult)
+        for hs in halves:
+            v = ang[:, hs].rearrange("p (t i) -> p t i", i=HALF)
+            nc.vector.tensor_tensor(out=v, in0=v, in1=freq[:].rearrange("p a b -> p (a b)").unsqueeze(1).to_broadcast([P, NT // 2, HALF]),
+                                    op=ALU.mult)
         for hs in halves:
             nc.vector.tensor_scalar(out=ni[:, hs], in0=ang[:, hs], scalar1=1.0 / TWO_PI, scalar2=None, op0=ALU.mult)
         for hs in halves:

@@ -50,6 +50,7 @@ def tile_multiheadselfattention_pa_kernel(tc, x_bytes, x_scale, w_aq, w_ak, out_
         ctx.enter_context(tc.manual_schedule())
 
         sc = keep.tile([P, KDIM], F32, name="sc")
+        sct = keep.tile([P, NG, 4], F32, name="sct")
         xby = keep.tile([P, NT * KDIM], U8, name="xby")
         ident = keep.tile([P, P], F32, name="ident")
         tab = keep.tile([P, NT, 2, 2, HALF], F32, name="tab")
@@ -59,7 +60,7 @@ def tile_multiheadselfattention_pa_kernel(tc, x_bytes, x_scale, w_aq, w_ak, out_
         wsc = keep.tile([P, NC * 512], U8, name="wsc", align_bytes=64)
         wraw_t = {}
 
-        nc.scalar.dma_start(out=sc[:], in_=x_scale.rearrange("a b k -> (a b k)").partition_broadcast(P))
+        nc.scalar.dma_start(out=sct[:], in_=x_scale.rearrange("a b (g p s) -> p (a b g) s", p=P, s=4))
 
         def load_x(t):
             nc.sync.dma_start(out=xby[:, t * KDIM:(t + 1) * KDIM], in_=xrows[t * P:(t + 1) * P, :])
@@ -77,6 +78,7 @@ def tile_multiheadselfattention_pa_kernel(tc, x_bytes, x_scale, w_aq, w_ak, out_
 
         load_x(0)
         load_x(1)
+        nc.sync.dma_start(out=sc[:], in_=x_scale.rearrange("a b k -> (a b k)").partition_broadcast(P))
         for t in range(2, NT):
             load_w(t - 2)
             load_x(t)
@@ -124,8 +126,10 @@ def tile_multiheadselfattention_pa_kernel(tc, x_bytes, x_scale, w_aq, w_ak, out_
             nc.vector.scalar_tensor_tensor(out=ang[:, hs], in0=nf[:, hs], scalar=-C2, in1=ang[:, hs], op0=ALU.mult, op1=ALU.add)
         for hs in halves:
             nc.vector.scalar_tensor_tensor(out=ra[:, hs], in0=ang[:, hs], scalar=-1.0, in1=ang[:, hs], op0=ALU.mult, op1=ALU.max)
-        nc.scalar.activation(out=sh[:].rearrange("p t i -> p (t i)"), in_=ang[:], func=ACT.Sin, scale=0.5)
-        nc.scalar.activation(out=ch[:].rearrange("p t i -> p (t i)"), in_=ra[:], func=ACT.Sin, scale=-0.5, bias=0.5 * PI)
+
+        def tables_sines():
+            nc.scalar.activation(out=sh[:].rearrange("p t i -> p (t i)"), in_=ang[:], func=ACT.Sin, scale=0.5)
+            nc.scalar.activation(out=ch[:].rearrange("p t i -> p (t i)"), in_=ra[:], func=ACT.Sin, scale=-0.5, bias=0.5 * PI)
 
         def tables_finish():
             nc.vector.scalar_tensor_tensor(out=tab[:, :, 1, 0, :], in0=sh[:], scalar=2.0, in1=ch[:], op0=ALU.mult, op1=ALU.mult)
@@ -149,6 +153,24 @@ def tile_multiheadselfattention_pa_kernel(tc, x_bytes, x_scale, w_aq, w_ak, out_
                                         in0=xby[:, t * KDIM + c * w:t * KDIM + (c + 1) * w].bitcast(FP8),
                                         in1=sc[:, c * w:(c + 1) * w], op=ALU.mult)
             xb_t[t] = xb
+
+        def x_cast(t):
+            xb = xbp.tile([P, KDIM], BF16, name="xb")
+            for g in range(NG):
+                nc.scalar.copy(out=xb[:, g * 512:(g + 1) * 512], in_=xby[:, t * KDIM + g * 512:t * KDIM + (g + 1) * 512].bitcast(FP8))
+            xb_t[t] = xb
+
+        def x_scale_out(t):
+            if t % 2 == 0:
+                xg = xgp.tile([P, 2 * KDIM], BF16, name="xg", align_bytes=64)
+                xg_t[t // 2] = xg
+            j = t % 2
+            dst = xg_t[t // 2][:, j * KDIM:(j + 1) * KDIM].rearrange("p (g r u e) -> p g r u e", g=NG, u=2, e=2)
+            for g in range(NG):
+                bank = xt_t[t][g // 2][:].bitcast(BF16).rearrange("p (g u r e) -> p g r u e", g=2, u=2, e=2)
+                nc.vector.tensor_tensor(out=dst[:, g], in0=bank[:, g % 2],
+                                        in1=sct[:, g].rearrange("p (u e) -> p u e", u=2).unsqueeze(1).to_broadcast([P, P, 2, 2]),
+                                        op=ALU.mult)
 
         def x_turn(t):
             words = xb_t[t][:].bitcast(F32)
@@ -237,13 +259,22 @@ def tile_multiheadselfattention_pa_kernel(tc, x_bytes, x_scale, w_aq, w_ak, out_
         VTILES = NQ * NT - 4
         LATE = 2
         issued = 0
+        EARLY = 2
+        x_cast(0)
+        tables_sines()
+        for t in range(1, EARLY):
+            x_cast(t)
         for t in range(NT):
-            x_product(t, 1)
+            if t >= EARLY:
+                x_product(t, 1)
             x_turn(t)
             if t < NT - LATE:
                 w_group(t)
                 load_w(t + 8)
-            x_copy(t)
+            if t >= EARLY:
+                x_copy(t)
+            else:
+                x_scale_out(t)
             if t == 0:
                 tables_finish()
             if t % 2 == 1 and t >= 3:

@@ -26,8 +26,6 @@ FLOPS = 2 * TOK * KDIM * 2 * HEADS * HD
 
 PI = 3.141592653589793
 TWO_PI = 2.0 * PI
-C1 = round(TWO_PI * 8192.0) / 8192.0
-C2 = TWO_PI - C1
 ROTARY_BASE = 10000.0
 
 
@@ -45,7 +43,7 @@ def tile_multiheadselfattention_pa_kernel(tc, x_bytes, x_scale, w_aq, w_ak, out_
         xbp = ctx.enter_context(tc.tile_pool(name="xbp", bufs=3))
         xgp = ctx.enter_context(tc.tile_pool(name="xgp", bufs=2))
         wgp = ctx.enter_context(tc.tile_pool(name="wgp", bufs=3))
-        abp = ctx.enter_context(tc.tile_pool(name="abp", bufs=4))
+        abp = ctx.enter_context(tc.tile_pool(name="abp", bufs=5))
         psum = ctx.enter_context(tc.psum_pool(name="psum", bufs=8))
         ctx.enter_context(tc.manual_schedule())
 
@@ -91,6 +89,7 @@ def tile_multiheadselfattention_pa_kernel(tc, x_bytes, x_scale, w_aq, w_ak, out_
         nc.scalar.activation(out=warm[:], in_=zero[:], func=ACT.Sin)
 
         ang = tmp.tile([P, NT * HALF], F32, name="ang")
+        pos = tmp.tile([P, NT], F32, name="pos")
         fparts = tmp.tile([P, 2, 8], F32, name="fparts")
         freq = tmp.tile([P, 8, 8], F32, name="freq")
         ni = tmp.tile([P, NT * HALF], I32, name="ni")
@@ -99,8 +98,7 @@ def tile_multiheadselfattention_pa_kernel(tc, x_bytes, x_scale, w_aq, w_ak, out_
         sh = tmp.tile([P, NT, HALF], F32, name="sh")
         ch = tmp.tile([P, NT, HALF], F32, name="ch")
         sq = tmp.tile([P, NT, HALF], F32, name="sq")
-        nc.gpsimd.iota(ang[:], pattern=[[P, NT], [0, HALF]], base=0, channel_multiplier=1,
-                       allow_small_or_imprecise_dtypes=True)
+        nc.gpsimd.iota(pos[:], pattern=[[P, NT]], base=0, channel_multiplier=1, allow_small_or_imprecise_dtypes=True)
         make_identity(nc, ident[:])
         W2 = NT * HALF // 2
         halves = [slice(0, W2), slice(W2, 2 * W2)]
@@ -112,18 +110,17 @@ def tile_multiheadselfattention_pa_kernel(tc, x_bytes, x_scale, w_aq, w_ak, out_
                 nc.vector.tensor_scalar(out=v, in0=v, scalar1=ROTARY_BASE ** (-low * step / 64.0), scalar2=None, op0=ALU.mult)
         nc.vector.tensor_tensor(out=freq[:], in0=fparts[:, 1].unsqueeze(2).to_broadcast([P, 8, 8]),
                                 in1=fparts[:, 0].unsqueeze(1).to_broadcast([P, 8, 8]), op=ALU.mult)
-        for hs in halves:
-            v = ang[:, hs].rearrange("p (t i) -> p t i", i=HALF)
-            nc.vector.tensor_tensor(out=v, in0=v, in1=freq[:].rearrange("p a b -> p (a b)").unsqueeze(1).to_broadcast([P, NT // 2, HALF]),
+        for c, hs in enumerate(halves):
+            nc.vector.tensor_tensor(out=ang[:, hs].rearrange("p (t i) -> p t i", i=HALF),
+                                    in0=pos[:, c * NT // 2:(c + 1) * NT // 2].unsqueeze(2).to_broadcast([P, NT // 2, HALF]),
+                                    in1=freq[:].rearrange("p a b -> p (a b)").unsqueeze(1).to_broadcast([P, NT // 2, HALF]),
                                     op=ALU.mult)
         for hs in halves:
             nc.vector.tensor_scalar(out=ni[:, hs], in0=ang[:, hs], scalar1=1.0 / TWO_PI, scalar2=None, op0=ALU.mult)
         for hs in halves:
             nc.vector.tensor_copy(out=nf[:, hs], in_=ni[:, hs])
         for hs in halves:
-            nc.vector.scalar_tensor_tensor(out=ang[:, hs], in0=nf[:, hs], scalar=-C1, in1=ang[:, hs], op0=ALU.mult, op1=ALU.add)
-        for hs in halves:
-            nc.vector.scalar_tensor_tensor(out=ang[:, hs], in0=nf[:, hs], scalar=-C2, in1=ang[:, hs], op0=ALU.mult, op1=ALU.add)
+            nc.vector.scalar_tensor_tensor(out=ang[:, hs], in0=nf[:, hs], scalar=-TWO_PI, in1=ang[:, hs], op0=ALU.mult, op1=ALU.add)
         for hs in halves:
             nc.vector.scalar_tensor_tensor(out=ra[:, hs], in0=ang[:, hs], scalar=-1.0, in1=ang[:, hs], op0=ALU.mult, op1=ALU.max)
 
@@ -205,8 +202,8 @@ def tile_multiheadselfattention_pa_kernel(tc, x_bytes, x_scale, w_aq, w_ak, out_
                 wg = wgp.tile([P, 2, 512, 4], BF16, name="wg", align_bytes=64)
                 wg_t[c // 2] = wg
             wg = wg_t[c // 2]
-            nc.scalar.copy(out=wg[:, c % 2].rearrange("p (h d) j -> p h d j", h=4),
-                           in_=wraw_t[c][:].rearrange("p h (j d) -> p h d j", j=4))
+            nc.scalar.copy(out=wg[:, c % 2].rearrange("p (h c i) j -> p h c j i", h=4, i=4),
+                           in_=wraw_t[c][:].rearrange("p h (j c i) -> p h c j i", j=4, i=4))
 
         def w_quant(k):
             lo = k * 1024

@@ -94,10 +94,10 @@ def tile_multiheadselfattention_pa_kernel(tc, x_bytes, x_scale, w_aq, w_ak, out_
         freq = tmp.tile([P, 8, 8], F32, name="freq")
         ni = tmp.tile([P, NT * HALF], I32, name="ni")
         nf = tmp.tile([P, NT * HALF], F32, name="nf")
-        ra = tmp.tile([P, NT * HALF], F32, name="ra")
         sh = tmp.tile([P, NT, HALF], F32, name="sh")
         ch = tmp.tile([P, NT, HALF], F32, name="ch")
         sq = tmp.tile([P, NT, HALF], F32, name="sq")
+        sq2 = tmp.tile([P, NT, HALF], F32, name="sq2")
         nc.gpsimd.iota(pos[:], pattern=[[P, NT]], base=0, channel_multiplier=1, allow_small_or_imprecise_dtypes=True)
         make_identity(nc, ident[:])
         W2 = NT * HALF // 2
@@ -121,17 +121,18 @@ def tile_multiheadselfattention_pa_kernel(tc, x_bytes, x_scale, w_aq, w_ak, out_
             nc.vector.tensor_copy(out=nf[:, hs], in_=ni[:, hs])
         for hs in halves:
             nc.vector.scalar_tensor_tensor(out=ang[:, hs], in0=nf[:, hs], scalar=-TWO_PI, in1=ang[:, hs], op0=ALU.mult, op1=ALU.add)
-        for hs in halves:
-            nc.vector.scalar_tensor_tensor(out=ra[:, hs], in0=ang[:, hs], scalar=-1.0, in1=ang[:, hs], op0=ALU.mult, op1=ALU.max)
 
         def tables_sines():
             nc.scalar.activation(out=sh[:].rearrange("p t i -> p (t i)"), in_=ang[:], func=ACT.Sin, scale=0.5)
-            nc.scalar.activation(out=ch[:].rearrange("p t i -> p (t i)"), in_=ra[:], func=ACT.Sin, scale=-0.5, bias=0.5 * PI)
+            nc.scalar.activation(out=ch[:].rearrange("p t i -> p (t i)"), in_=ang[:], func=ACT.Sin, scale=0.5, bias=-0.25 * PI)
 
         def tables_finish():
-            nc.vector.scalar_tensor_tensor(out=tab[:, :, 1, 0, :], in0=sh[:], scalar=2.0, in1=ch[:], op0=ALU.mult, op1=ALU.mult)
-            nc.vector.tensor_tensor(out=sq[:], in0=sh[:], in1=sh[:], op=ALU.mult)
-            nc.scalar.activation(out=tab[:, :, 1, 1, :], in_=tab[:, :, 1, 0, :], func=ACT.Copy, scale=-1.0)
+            nc.scalar.activation(out=sq[:], in_=sh[:], func=ACT.Square)
+            nc.scalar.activation(out=sq2[:], in_=ch[:], func=ACT.Square)
+
+        def tables_write():
+            nc.scalar.activation(out=tab[:, :, 1, 0, :], in_=sq2[:], func=ACT.Copy, scale=-2.0, bias=1.0)
+            nc.scalar.activation(out=tab[:, :, 1, 1, :], in_=sq2[:], func=ACT.Copy, scale=2.0, bias=-1.0)
             nc.scalar.activation(out=tab[:, :, 0, :, :], in_=sq[:].unsqueeze(2).to_broadcast([P, NT, 2, HALF]),
                                  func=ACT.Copy, scale=-2.0, bias=1.0)
 
@@ -257,23 +258,24 @@ def tile_multiheadselfattention_pa_kernel(tc, x_bytes, x_scale, w_aq, w_ak, out_
         LATE = 2
         issued = 0
         EARLY = 2
-        x_cast(0)
-        tables_sines()
-        for t in range(1, EARLY):
+        for t in range(EARLY):
             x_cast(t)
+        tables_sines()
         for t in range(NT):
             if t >= EARLY:
                 x_product(t, 1)
             x_turn(t)
-            if t < NT - LATE:
-                w_group(t)
-                load_w(t + 8)
             if t >= EARLY:
                 x_copy(t)
             else:
                 x_scale_out(t)
             if t == 0:
                 tables_finish()
+            if t < NT - LATE:
+                w_group(t)
+                load_w(t + 8)
+            if t == NT - LATE - 1:
+                tables_write()
             if t % 2 == 1 and t >= 3:
                 w_quant(t // 2 - 1)
                 x_quant(t // 2 - 1)

@@ -255,6 +255,7 @@ def tile_multiheadselfattention_pa_kernel(tc, x_bytes, x_scale, w_aq, w_ak, out_
 
         AHEAD = 2
         VTILES = NQ * NT - 4
+        VLAG = 2
         LATE = 2
         issued = 0
         EARLY = 2
@@ -301,8 +302,9 @@ def tile_multiheadselfattention_pa_kernel(tc, x_bytes, x_scale, w_aq, w_ak, out_
                 products(issued)
                 issued += 1
             rotate(i)
-            if i > VTILES:
-                finish_tile(i - 1)
+            if i >= VTILES + VLAG:
+                finish_tile(i - VLAG)
             elif i % 2 == 1 and i < VTILES:
                 finish(i // 2)
-        finish_tile(NQ * NT - 1)
+        for i in range(NQ * NT - VLAG, NQ * NT):
+            finish_tile(i)

@@ -203,8 +203,8 @@ def tile_multiheadselfattention_pa_kernel(tc, x_bytes, x_scale, w_aq, w_ak, out_
                 wg = wgp.tile([P, 2, 512, 4], BF16, name="wg", align_bytes=64)
                 wg_t[c // 2] = wg
             wg = wg_t[c // 2]
-            nc.scalar.copy(out=wg[:, c % 2].rearrange("p (h c i) j -> p h c j i", h=4, i=4),
-                           in_=wraw_t[c][:].rearrange("p h (j c i) -> p h c j i", j=4, i=4))
+            nc.scalar.copy(out=wg[:, c % 2].rearrange("p (h c i) j -> p h c j i", h=4, i=8),
+                           in_=wraw_t[c][:].rearrange("p h (j c i) -> p h c j i", j=4, i=8))
 
         def w_quant(k):
             lo = k * 1024

@@ -22,6 +22,7 @@ HALF = 64
 NT = TOK // P
 NG = KDIM // 512
 NQ = 4
+NB = 5
 FLOPS = 2 * TOK * KDIM * 2 * HEADS * HD
 
 PI = 3.141592653589793
@@ -43,7 +44,7 @@ def tile_multiheadselfattention_pa_kernel(tc, x_bytes, x_scale, w_aq, w_ak, out_
         xbp = ctx.enter_context(tc.tile_pool(name="xbp", bufs=3))
         xgp = ctx.enter_context(tc.tile_pool(name="xgp", bufs=2))
         wgp = ctx.enter_context(tc.tile_pool(name="wgp", bufs=3))
-        abp = ctx.enter_context(tc.tile_pool(name="abp", bufs=5))
+        abp = ctx.enter_context(tc.tile_pool(name="abp", bufs=NB))
         psum = ctx.enter_context(tc.psum_pool(name="psum", bufs=8))
         ctx.enter_context(tc.manual_schedule())
 
@@ -51,6 +52,8 @@ def tile_multiheadselfattention_pa_kernel(tc, x_bytes, x_scale, w_aq, w_ak, out_
         sct = keep.tile([P, NG, 4], F32, name="sct")
         xby = keep.tile([P, NT * KDIM], U8, name="xby")
         ident = keep.tile([P, P], F32, name="ident")
+        swap = keep.tile([P, P], F32, name="swap")
+        tabt = keep.tile([P, 2, 2 * P], F32, name="tabt")
         tab = keep.tile([P, NT, 2, 2, HALF], F32, name="tab")
         xc = keep.tile([P, NT * NG * P], U32, name="xc", align_bytes=64)
         xs = keep.tile([P, NT * NG * P], U8, name="xs", align_bytes=64)
@@ -163,7 +166,7 @@ def tile_multiheadselfattention_pa_kernel(tc, x_bytes, x_scale, w_aq, w_ak, out_
                 xg = xgp.tile([P, 2 * KDIM], BF16, name="xg", align_bytes=64)
                 xg_t[t // 2] = xg
             j = t % 2
-            dst = xg_t[t // 2][:, j * KDIM:(j + 1) * KDIM].rearrange("p (g r u e) -> p g r u e", g=NG, u=2, e=2)
+            dst = xg_t[t // 2][:].rearrange("p (g j r u e) -> p g j r u e", g=NG, j=2, u=2, e=2)[:, :, j]
             for g in range(NG):
                 bank = xt_t[t][g // 2][:].bitcast(BF16).rearrange("p (g u r e) -> p g r u e", g=2, u=2, e=2)
                 nc.vector.tensor_tensor(out=dst[:, g], in0=bank[:, g % 2],
@@ -189,7 +192,7 @@ def tile_multiheadselfattention_pa_kernel(tc, x_bytes, x_scale, w_aq, w_ak, out_
                 xg_t[t // 2] = xg
             xg = xg_t[t // 2]
             j = t % 2
-            xgw = xg[:, j * KDIM:(j + 1) * KDIM].bitcast(F32).rearrange("p (g r u) -> p g r u", g=NG, u=2)
+            xgw = xg[:].bitcast(F32).rearrange("p (g j r u) -> p g j r u", g=NG, j=2, u=2)[:, :, j]
             for b in range(2):
                 nc.scalar.copy(out=xgw[:, 2 * b:2 * b + 2], in_=xt_t[t][b][:].rearrange("p (g u r) -> p g r u", g=2, u=2))
 
@@ -212,55 +215,120 @@ def tile_multiheadselfattention_pa_kernel(tc, x_bytes, x_scale, w_aq, w_ak, out_
                                   in_=wg_t[k][:].rearrange("p e c j -> p (e c j)"))
 
         def products(i):
-            q, t = divmod(i, NT)
+            m, j = divmod(i, 2)
+            q, k = jobs[m]
             ps = psum.tile([P, 512], F32, name="ps", tag="bank")
             ps_t[i] = ps
+            if m in TURNED:
+                for h in range(2):
+                    for g in range(NG):
+                        xo = (k * NG + g) * 2 * P
+                        wo = (q * NG + g) * 512 + (2 * j + h) * HD
+                        nc.tensor.matmul_mx(out=ps[:, h * 256:(h + 1) * 256], lhsT=wc[:, wo:wo + HD].bitcast(FP8X4), lhsT_scale=wsc[:, wo:wo + HD],
+                                            rhs=xc[:, xo:xo + 2 * P].bitcast(FP8X4), rhs_scale=xs[:, xo:xo + 2 * P],
+                                            start=(g == 0), stop=(g == NG - 1))
+                if j == 0:
+                    ab = abp.tile([P, 2, 2, 4, HD], F32, name="ab")
+                    ab_t[m] = ab
+                if m in VBOTH:
+                    return
+                nc.scalar.copy(out=ab_t[m][:, 1, j].rearrange("p h d -> p (h d)"), in_=ps[:])
+                if j == 1:
+                    b = ab_t[m][:, 1].rearrange("p j (h b) d -> p (j h) (b d)", h=2)
+                    nc.gpsimd.tensor_tensor(out=b, in0=b, in1=tabt[:, 1].unsqueeze(1).to_broadcast([P, 4, 2 * P]), op=ALU.mult)
+                return
             for g in range(NG):
-                xo = (t * NG + g) * P
+                xo = (k * NG + g) * 2 * P + j * P
                 wo = (q * NG + g) * 512
                 nc.tensor.matmul_mx(out=ps[:], lhsT=xc[:, xo:xo + P].bitcast(FP8X4), lhsT_scale=xs[:, xo:xo + P],
                                     rhs=wc[:, wo:wo + 512].bitcast(FP8X4), rhs_scale=wsc[:, wo:wo + 512],
                                     start=(g == 0), stop=(g == NG - 1))
 
         def rotate(i):
-            t = i % NT
-            if i % 2 == 0:
+            m, j = divmod(i, 2)
+            k = jobs[m][1]
+            if m in VBOTH:
+                nc.vector.tensor_tensor(out=ab_t[m][:, :, j].rearrange("p r (h b) d -> p r h (b d)", h=2),
+                                        in0=ps_t[i][:].rearrange("p (h t) -> p h t", h=2).unsqueeze(1).to_broadcast([P, 2, 2, 2 * P]),
+                                        in1=tabt[:].unsqueeze(2).to_broadcast([P, 2, 2, 2 * P]), op=ALU.mult)
+                return
+            if m in TURNED:
+                nc.vector.tensor_tensor(out=ab_t[m][:, 0, j].rearrange("p (h b) d -> p h (b d)", h=2),
+                                        in0=ps_t[i][:].rearrange("p (h t) -> p h t", h=2),
+                                        in1=tabt[:, 0].unsqueeze(1).to_broadcast([P, 2, 2 * P]), op=ALU.mult)
+                return
+            if j == 0:
                 ab = abp.tile([P, 2, 2, 4, HD], F32, name="ab")
-                ab_t[i // 2] = ab
+                ab_t[m] = ab
             nc.vector.tensor_tensor(
-                out=ab_t[i // 2][:, :, i % 2],
+                out=ab_t[m][:, :, j],
                 in0=ps_t[i][:].rearrange("p (h d) -> p h d", h=4).unsqueeze(1).to_broadcast([P, 2, 4, HD]),
-                in1=tab[:, t].rearrange("p r f i -> p r (f i)").unsqueeze(2).to_broadcast([P, 2, 4, HD]),
+                in1=tab[:, 2 * k + j].rearrange("p r f i -> p r (f i)").unsqueeze(2).to_broadcast([P, 2, 4, HD]),
                 op=ALU.mult,
             )
 
-        def finish(k):
-            q, tp = divmod(k, NT // 2)
-            ab = ab_t[k]
-            dst = outs[q // 2][2 * tp * P:(2 * tp + 2) * P, (q % 2) * 512:(q % 2 + 1) * 512].rearrange("(j p) c -> p j c", p=P)
+        def store(m):
+            q, k = jobs[m]
+            dst = outs[q // 2][2 * k * P:(2 * k + 2) * P, (q % 2) * 512:(q % 2 + 1) * 512].rearrange("(j p) c -> p j c", p=P)
+            nc.sync.dma_start(out=dst, in_=ab_t[m][:, 0].rearrange("p j h d -> p j (h d)"))
+
+        def finish(m):
+            ab = ab_t[m]
+            if m in TURNED:
+                return
             a0 = ab[:, 0].rearrange("p j h (f i) -> p (j h) f i", f=2)
             a1 = ab[:, 1].rearrange("p j h (f i) -> p (j h) f i", f=2)[:, :, ::-1, :]
             nc.gpsimd.tensor_tensor(out=a0, in0=a0, in1=a1, op=ALU.add)
-            nc.sync.dma_start(out=dst, in_=ab[:, 0].rearrange("p j h d -> p j (h d)"))
+            store(m)
+
+        def turn_back(m):
+            ab = ab_t[m]
+            banks = []
+            for b in range(2):
+                res = psum.tile([P, 512], F32, name="res", tag="bank")
+                banks.append(res)
+                for h in range(4):
+                    blk = (h % 2) * 2 + b
+                    nc.tensor.matmul(out=res[:, h * HD:(h + 1) * HD], lhsT=ab[:, 0, h // 2, blk], rhs=ident[:], start=True, stop=False, is_transpose=True)
+                    nc.tensor.matmul(out=res[:, h * HD:(h + 1) * HD], lhsT=ab[:, 1, h // 2, blk], rhs=swap[:], start=False, stop=True, is_transpose=True)
+            for b in range(2):
+                nc.scalar.copy(out=ab[:, 0, b].rearrange("p h d -> p (h d)"), in_=banks[b][:])
+            store(m)
 
         def finish_tile(i):
-            k, j = divmod(i, 2)
-            q, tp = divmod(k, NT // 2)
-            ab = ab_t[k]
-            dst = outs[q // 2][i % NT * P:(i % NT + 1) * P, (q % 2) * 512:(q % 2 + 1) * 512]
+            m, j = divmod(i, 2)
+            q, k = jobs[m]
+            ab = ab_t[m]
+            t = 2 * k + j
+            dst = outs[q // 2][t * P:(t + 1) * P, (q % 2) * 512:(q % 2 + 1) * 512]
             a0 = ab[:, 0, j].rearrange("p h (f i) -> p h f i", f=2)
             a1 = ab[:, 1, j].rearrange("p h (f i) -> p h f i", f=2)[:, :, ::-1, :]
             nc.vector.tensor_tensor(out=a0, in0=a0, in1=a1, op=ALU.add)
             nc.sync.dma_start(out=dst, in_=ab[:, 0, j].rearrange("p h d -> p (h d)"))
 
+        def tables_turn(k):
+            tt = psum.tile([P, 2, 2, P], F32, name="tt", tag="bank")
+            for r in range(2):
+                for j in range(2):
+                    nc.tensor.transpose(tt[:, r, j], tab[:, 2 * k + j, r].rearrange("p f i -> p (f i)"), ident[:])
+            nc.scalar.copy(out=tabt[:].rearrange("p r t -> p (r t)"), in_=tt[:].rearrange("p r j t -> p (r j t)"))
+
+        jobs = [(q, k) for q in range(NQ) for k in range(NT // 2)]
+        TK = 1
+        WQ = {6: 3, 10: 4, 14: 5, 18: 6, 22: 7}
+        TB = 0
+        TURNED = (5, 9, 13)
+        VBOTH = (5, 9, 13)
         AHEAD = 2
-        VTILES = NQ * NT - 4
+        VTILES = 30
         VLAG = 2
         LATE = 2
         issued = 0
         EARLY = 2
         for t in range(EARLY):
             x_cast(t)
+        nc.gpsimd.tensor_copy(out=swap[:, 0:HALF], in_=ident[:, HALF:P])
+        nc.gpsimd.tensor_copy(out=swap[:, HALF:P], in_=ident[:, 0:HALF])
         tables_sines()
         for t in range(NT):
             if t >= EARLY:
@@ -284,6 +352,7 @@ def tile_multiheadselfattention_pa_kernel(tc, x_bytes, x_scale, w_aq, w_ak, out_
                 products(issued)
                 products(issued + 1)
                 issued += 2
+        tables_turn(TK)
 
         grouped = NT - LATE
         for i in range(NQ * NT):
@@ -296,12 +365,14 @@ def tile_multiheadselfattention_pa_kernel(tc, x_bytes, x_scale, w_aq, w_ak, out_
                 grouped += 1
             if i == 2:
                 x_quant(3)
-            elif i % 4 == 2 and i <= 22:
-                w_quant(2 + i // 4)
+            elif i in WQ:
+                w_quant(WQ[i])
             while issued < NQ * NT and issued <= i + AHEAD:
                 products(issued)
                 issued += 1
             rotate(i)
+            if i % 2 == TB and i // 2 - 1 in TURNED:
+                turn_back(i // 2 - 1)
             if i >= VTILES + VLAG:
                 finish_tile(i - VLAG)
             elif i % 2 == 1 and i < VTILES:

@@ -20,9 +20,10 @@ HEADS = 8
 HD = 128
 HALF = 64
 NT = TOK // P
+NK = NT // 2
 NG = KDIM // 512
 NQ = 4
-NB = 5
+NC = NQ * NG
 FLOPS = 2 * TOK * KDIM * 2 * HEADS * HD
 
 PI = 3.141592653589793
@@ -35,7 +36,9 @@ def tile_multiheadselfattention_pa_kernel(tc, x_bytes, x_scale, w_aq, w_ak, out_
     xrows = x_bytes.flatten_outer_dims()
     outs = [out_0.rearrange("b t h d -> (b t) (h d)"), out_1.rearrange("b t h d -> (b t) (h d)")]
     ws_in = [w_aq, w_ak]
-    NC = NQ * NG
+
+    TURNED = (1, 4, 9, 13)
+    W_AT = {5: 3, 11: 4, 12: 5, 21: 6, 22: 7}
 
     with ExitStack() as ctx:
         keep = ctx.enter_context(tc.tile_pool(name="keep", bufs=1))
@@ -44,7 +47,7 @@ def tile_multiheadselfattention_pa_kernel(tc, x_bytes, x_scale, w_aq, w_ak, out_
         xbp = ctx.enter_context(tc.tile_pool(name="xbp", bufs=3))
         xgp = ctx.enter_context(tc.tile_pool(name="xgp", bufs=2))
         wgp = ctx.enter_context(tc.tile_pool(name="wgp", bufs=3))
-        abp = ctx.enter_context(tc.tile_pool(name="abp", bufs=NB))
+        abp = ctx.enter_context(tc.tile_pool(name="abp", bufs=5))
         psum = ctx.enter_context(tc.psum_pool(name="psum", bufs=8))
         ctx.enter_context(tc.manual_schedule())
 
@@ -53,8 +56,8 @@ def tile_multiheadselfattention_pa_kernel(tc, x_bytes, x_scale, w_aq, w_ak, out_
         xby = keep.tile([P, NT * KDIM], U8, name="xby")
         ident = keep.tile([P, P], F32, name="ident")
         swap = keep.tile([P, P], F32, name="swap")
-        tabt = keep.tile([P, 2, 2 * P], F32, name="tabt")
         tab = keep.tile([P, NT, 2, 2, HALF], F32, name="tab")
+        tabt = keep.tile([P, 2, 2, 2 * P], F32, name="tabt")
         xc = keep.tile([P, NT * NG * P], U32, name="xc", align_bytes=64)
         xs = keep.tile([P, NT * NG * P], U8, name="xs", align_bytes=64)
         wc = keep.tile([P, NC * 512], U32, name="wc", align_bytes=64)
@@ -79,12 +82,16 @@ def tile_multiheadselfattention_pa_kernel(tc, x_bytes, x_scale, w_aq, w_ak, out_
 
         load_x(0)
         load_x(1)
+        load_w(0)
+        load_w(1)
+        load_x(2)
         nc.sync.dma_start(out=sc[:], in_=x_scale.rearrange("a b k -> (a b k)").partition_broadcast(P))
-        for t in range(2, NT):
-            load_w(t - 2)
+        load_x(3)
+        load_w(2)
+        load_w(3)
+        for t in range(4, NT):
             load_x(t)
-        load_w(6)
-        load_w(7)
+            load_w(t)
 
         zero = tmp.tile([P, 1], F32, name="zero")
         warm = tmp.tile([P, 1], F32, name="warm")
@@ -128,8 +135,6 @@ def tile_multiheadselfattention_pa_kernel(tc, x_bytes, x_scale, w_aq, w_ak, out_
         def tables_sines():
             nc.scalar.activation(out=sh[:].rearrange("p t i -> p (t i)"), in_=ang[:], func=ACT.Sin, scale=0.5)
             nc.scalar.activation(out=ch[:].rearrange("p t i -> p (t i)"), in_=ang[:], func=ACT.Sin, scale=0.5, bias=-0.25 * PI)
-
-        def tables_finish():
             nc.scalar.activation(out=sq[:], in_=sh[:], func=ACT.Square)
             nc.scalar.activation(out=sq2[:], in_=ch[:], func=ACT.Square)
 
@@ -139,6 +144,10 @@ def tile_multiheadselfattention_pa_kernel(tc, x_bytes, x_scale, w_aq, w_ak, out_
             nc.scalar.activation(out=tab[:, :, 0, :, :], in_=sq[:].unsqueeze(2).to_broadcast([P, NT, 2, HALF]),
                                  func=ACT.Copy, scale=-2.0, bias=1.0)
 
+        def swap_write():
+            nc.scalar.copy(out=swap[:, 0:HALF], in_=ident[:, HALF:P])
+            nc.scalar.copy(out=swap[:, HALF:P], in_=ident[:, 0:HALF])
+
         xb_t = {}
         xg_t = {}
         xt_t = {}
@@ -146,32 +155,21 @@ def tile_multiheadselfattention_pa_kernel(tc, x_bytes, x_scale, w_aq, w_ak, out_
         ab_t = {}
         wg_t = {}
 
-        def x_product(t, pieces):
+        def x_product(t):
             xb = xbp.tile([P, KDIM], BF16, name="xb")
-            w = KDIM // pieces
-            for c in range(pieces):
-                nc.vector.tensor_tensor(out=xb[:, c * w:(c + 1) * w],
-                                        in0=xby[:, t * KDIM + c * w:t * KDIM + (c + 1) * w].bitcast(FP8),
-                                        in1=sc[:, c * w:(c + 1) * w], op=ALU.mult)
+            nc.vector.tensor_tensor(out=xb[:], in0=xby[:, t * KDIM:(t + 1) * KDIM].bitcast(FP8), in1=sc[:], op=ALU.mult)
             xb_t[t] = xb
 
-        def x_cast(t):
+        def x_cast(t, vector_from=NG):
             xb = xbp.tile([P, KDIM], BF16, name="xb")
             for g in range(NG):
-                nc.scalar.copy(out=xb[:, g * 512:(g + 1) * 512], in_=xby[:, t * KDIM + g * 512:t * KDIM + (g + 1) * 512].bitcast(FP8))
+                out = xb[:, g * 512:(g + 1) * 512]
+                codes = xby[:, t * KDIM + g * 512:t * KDIM + (g + 1) * 512].bitcast(FP8)
+                if g >= vector_from:
+                    nc.vector.tensor_copy(out=out, in_=codes)
+                else:
+                    nc.scalar.copy(out=out, in_=codes)
             xb_t[t] = xb
-
-        def x_scale_out(t):
-            if t % 2 == 0:
-                xg = xgp.tile([P, 2 * KDIM], BF16, name="xg", align_bytes=64)
-                xg_t[t // 2] = xg
-            j = t % 2
-            dst = xg_t[t // 2][:].rearrange("p (g j r u e) -> p g j r u e", g=NG, j=2, u=2, e=2)[:, :, j]
-            for g in range(NG):
-                bank = xt_t[t][g // 2][:].bitcast(BF16).rearrange("p (g u r e) -> p g r u e", g=2, u=2, e=2)
-                nc.vector.tensor_tensor(out=dst[:, g], in0=bank[:, g % 2],
-                                        in1=sct[:, g].rearrange("p (u e) -> p u e", u=2).unsqueeze(1).to_broadcast([P, P, 2, 2]),
-                                        op=ALU.mult)
 
         def x_turn(t):
             words = xb_t[t][:].bitcast(F32)
@@ -186,15 +184,24 @@ def tile_multiheadselfattention_pa_kernel(tc, x_bytes, x_scale, w_aq, w_ak, out_
                                             words[:, 256 * g + u:256 * (g + 1):2], ident[:])
             xt_t[t] = banks
 
-        def x_copy(t):
+        def x_pair_tile(t):
             if t % 2 == 0:
                 xg = xgp.tile([P, 2 * KDIM], BF16, name="xg", align_bytes=64)
                 xg_t[t // 2] = xg
-            xg = xg_t[t // 2]
-            j = t % 2
-            xgw = xg[:].bitcast(F32).rearrange("p (g j r u) -> p g j r u", g=NG, j=2, u=2)[:, :, j]
+            return xg_t[t // 2]
+
+        def x_scale_out(t):
+            dst = x_pair_tile(t)[:].rearrange("p (g j r u e) -> p g j r u e", g=NG, j=2, u=2, e=2)[:, :, t % 2]
+            for g in range(NG):
+                bank = xt_t[t][g // 2][:].bitcast(BF16).rearrange("p (g u r e) -> p g r u e", g=2, u=2, e=2)
+                nc.vector.tensor_tensor(out=dst[:, g], in0=bank[:, g % 2],
+                                        in1=sct[:, g].rearrange("p (u e) -> p u e", u=2).unsqueeze(1).to_broadcast([P, P, 2, 2]),
+                                        op=ALU.mult)
+
+        def x_copy(t):
+            dst = x_pair_tile(t)[:].bitcast(F32).rearrange("p (g j r u) -> p g j r u", g=NG, j=2, u=2)[:, :, t % 2]
             for b in range(2):
-                nc.scalar.copy(out=xgw[:, 2 * b:2 * b + 2], in_=xt_t[t][b][:].rearrange("p (g u r) -> p g r u", g=2, u=2))
+                nc.scalar.copy(out=dst[:, 2 * b:2 * b + 2], in_=xt_t[t][b][:].rearrange("p (g u r) -> p g r u", g=2, u=2))
 
         def x_quant(k):
             lo = k * 2 * NG * P
@@ -208,6 +215,8 @@ def tile_multiheadselfattention_pa_kernel(tc, x_bytes, x_scale, w_aq, w_ak, out_
             wg = wg_t[c // 2]
             nc.scalar.copy(out=wg[:, c % 2].rearrange("p (h c i) j -> p h c j i", h=4, i=8),
                            in_=wraw_t[c][:].rearrange("p h (j c i) -> p h c j i", j=4, i=8))
+            if c + 8 < NC:
+                load_w(c + 8)
 
         def w_quant(k):
             lo = k * 1024
@@ -216,7 +225,7 @@ def tile_multiheadselfattention_pa_kernel(tc, x_bytes, x_scale, w_aq, w_ak, out_
 
         def products(i):
             m, j = divmod(i, 2)
-            q, k = jobs[m]
+            q, k = divmod(m, NK)
             ps = psum.tile([P, 512], F32, name="ps", tag="bank")
             ps_t[i] = ps
             if m in TURNED:
@@ -224,18 +233,10 @@ def tile_multiheadselfattention_pa_kernel(tc, x_bytes, x_scale, w_aq, w_ak, out_
                     for g in range(NG):
                         xo = (k * NG + g) * 2 * P
                         wo = (q * NG + g) * 512 + (2 * j + h) * HD
-                        nc.tensor.matmul_mx(out=ps[:, h * 256:(h + 1) * 256], lhsT=wc[:, wo:wo + HD].bitcast(FP8X4), lhsT_scale=wsc[:, wo:wo + HD],
+                        nc.tensor.matmul_mx(out=ps[:, h * 2 * P:(h + 1) * 2 * P],
+                                            lhsT=wc[:, wo:wo + HD].bitcast(FP8X4), lhsT_scale=wsc[:, wo:wo + HD],
                                             rhs=xc[:, xo:xo + 2 * P].bitcast(FP8X4), rhs_scale=xs[:, xo:xo + 2 * P],
                                             start=(g == 0), stop=(g == NG - 1))
-                if j == 0:
-                    ab = abp.tile([P, 2, 2, 4, HD], F32, name="ab")
-                    ab_t[m] = ab
-                if m in VBOTH:
-                    return
-                nc.scalar.copy(out=ab_t[m][:, 1, j].rearrange("p h d -> p (h d)"), in_=ps[:])
-                if j == 1:
-                    b = ab_t[m][:, 1].rearrange("p j (h b) d -> p (j h) (b d)", h=2)
-                    nc.gpsimd.tensor_tensor(out=b, in0=b, in1=tabt[:, 1].unsqueeze(1).to_broadcast([P, 4, 2 * P]), op=ALU.mult)
                 return
             for g in range(NG):
                 xo = (k * NG + g) * 2 * P + j * P
@@ -246,36 +247,33 @@ def tile_multiheadselfattention_pa_kernel(tc, x_bytes, x_scale, w_aq, w_ak, out_
 
         def rotate(i):
             m, j = divmod(i, 2)
-            k = jobs[m][1]
-            if m in VBOTH:
-                nc.vector.tensor_tensor(out=ab_t[m][:, :, j].rearrange("p r (h b) d -> p r h (b d)", h=2),
-                                        in0=ps_t[i][:].rearrange("p (h t) -> p h t", h=2).unsqueeze(1).to_broadcast([P, 2, 2, 2 * P]),
-                                        in1=tabt[:].unsqueeze(2).to_broadcast([P, 2, 2, 2 * P]), op=ALU.mult)
-                return
-            if m in TURNED:
-                nc.vector.tensor_tensor(out=ab_t[m][:, 0, j].rearrange("p (h b) d -> p h (b d)", h=2),
-                                        in0=ps_t[i][:].rearrange("p (h t) -> p h t", h=2),
-                                        in1=tabt[:, 0].unsqueeze(1).to_broadcast([P, 2, 2 * P]), op=ALU.mult)
-                return
+            k = m % NK
             if j == 0:
                 ab = abp.tile([P, 2, 2, 4, HD], F32, name="ab")
                 ab_t[m] = ab
+            ab = ab_t[m]
+            if m in TURNED:
+                nc.vector.tensor_tensor(
+                    out=ab[:, :, j].rearrange("p r (h b) d -> p r h (b d)", h=2),
+                    in0=ps_t[i][:].rearrange("p (h t) -> p h t", h=2).unsqueeze(1).to_broadcast([P, 2, 2, 2 * P]),
+                    in1=tabt[:, k].unsqueeze(2).to_broadcast([P, 2, 2, 2 * P]),
+                    op=ALU.mult,
+                )
+                return
             nc.vector.tensor_tensor(
-                out=ab_t[m][:, :, j],
+                out=ab[:, :, j],
                 in0=ps_t[i][:].rearrange("p (h d) -> p h d", h=4).unsqueeze(1).to_broadcast([P, 2, 4, HD]),
                 in1=tab[:, 2 * k + j].rearrange("p r f i -> p r (f i)").unsqueeze(2).to_broadcast([P, 2, 4, HD]),
                 op=ALU.mult,
             )
 
         def store(m):
-            q, k = jobs[m]
+            q, k = divmod(m, NK)
             dst = outs[q // 2][2 * k * P:(2 * k + 2) * P, (q % 2) * 512:(q % 2 + 1) * 512].rearrange("(j p) c -> p j c", p=P)
             nc.sync.dma_start(out=dst, in_=ab_t[m][:, 0].rearrange("p j h d -> p j (h d)"))
 
         def finish(m):
             ab = ab_t[m]
-            if m in TURNED:
-                return
             a0 = ab[:, 0].rearrange("p j h (f i) -> p (j h) f i", f=2)
             a1 = ab[:, 1].rearrange("p j h (f i) -> p (j h) f i", f=2)[:, :, ::-1, :]
             nc.gpsimd.tensor_tensor(out=a0, in0=a0, in1=a1, op=ALU.add)
@@ -284,20 +282,21 @@ def tile_multiheadselfattention_pa_kernel(tc, x_bytes, x_scale, w_aq, w_ak, out_
         def turn_back(m):
             ab = ab_t[m]
             banks = []
-            for b in range(2):
+            for j in range(2):
                 res = psum.tile([P, 512], F32, name="res", tag="bank")
                 banks.append(res)
                 for h in range(4):
-                    blk = (h % 2) * 2 + b
-                    nc.tensor.matmul(out=res[:, h * HD:(h + 1) * HD], lhsT=ab[:, 0, h // 2, blk], rhs=ident[:], start=True, stop=False, is_transpose=True)
-                    nc.tensor.matmul(out=res[:, h * HD:(h + 1) * HD], lhsT=ab[:, 1, h // 2, blk], rhs=swap[:], start=False, stop=True, is_transpose=True)
-            for b in range(2):
-                nc.scalar.copy(out=ab[:, 0, b].rearrange("p h d -> p (h d)"), in_=banks[b][:])
+                    out = res[:, h * HD:(h + 1) * HD]
+                    block = (h % 2) * 2 + j
+                    nc.tensor.matmul(out=out, lhsT=ab[:, 0, h // 2, block], rhs=ident[:], start=True, stop=False, is_transpose=True)
+                    nc.tensor.matmul(out=out, lhsT=ab[:, 1, h // 2, block], rhs=swap[:], start=False, stop=True, is_transpose=True)
+            for j in range(2):
+                nc.scalar.copy(out=ab[:, 0, j].rearrange("p h d -> p (h d)"), in_=banks[j][:])
             store(m)
 
         def finish_tile(i):
             m, j = divmod(i, 2)
-            q, k = jobs[m]
+            q, k = divmod(m, NK)
             ab = ab_t[m]
             t = 2 * k + j
             dst = outs[q // 2][t * P:(t + 1) * P, (q % 2) * 512:(q % 2 + 1) * 512]
@@ -311,71 +310,63 @@ def tile_multiheadselfattention_pa_kernel(tc, x_bytes, x_scale, w_aq, w_ak, out_
             for r in range(2):
                 for j in range(2):
                     nc.tensor.transpose(tt[:, r, j], tab[:, 2 * k + j, r].rearrange("p f i -> p (f i)"), ident[:])
-            nc.scalar.copy(out=tabt[:].rearrange("p r t -> p (r t)"), in_=tt[:].rearrange("p r j t -> p (r j t)"))
+            nc.scalar.copy(out=tabt[:, k].rearrange("p r t -> p (r t)"), in_=tt[:].rearrange("p r j t -> p (r j t)"))
 
-        jobs = [(q, k) for q in range(NQ) for k in range(NT // 2)]
-        TK = 1
-        WQ = {6: 3, 10: 4, 14: 5, 18: 6, 22: 7}
-        TB = 0
-        TURNED = (5, 9, 13)
-        VBOTH = (5, 9, 13)
-        AHEAD = 2
-        VTILES = 30
-        VLAG = 2
+        EARLY = 3
         LATE = 2
+        AHEAD = 2
         issued = 0
-        EARLY = 2
-        for t in range(EARLY):
-            x_cast(t)
-        nc.gpsimd.tensor_copy(out=swap[:, 0:HALF], in_=ident[:, HALF:P])
-        nc.gpsimd.tensor_copy(out=swap[:, HALF:P], in_=ident[:, 0:HALF])
+        x_cast(0, vector_from=2)
+        x_cast(1)
+        x_turn(0)
+        x_scale_out(0)
+        w_group(0)
+        x_turn(1)
+        x_scale_out(1)
+        w_group(1)
+        x_cast(2)
         tables_sines()
-        for t in range(NT):
-            if t >= EARLY:
-                x_product(t, 1)
+        w_quant(0)
+        x_turn(2)
+        x_scale_out(2)
+        swap_write()
+        for t in range(EARLY, NT):
+            x_product(t)
             x_turn(t)
-            if t >= EARLY:
-                x_copy(t)
-            else:
-                x_scale_out(t)
-            if t == 0:
-                tables_finish()
-            if t < NT - LATE:
-                w_group(t)
-                load_w(t + 8)
+            if t - 1 < NT - LATE:
+                w_group(t - 1)
+            x_copy(t)
+            if t == EARLY:
+                x_quant(0)
             if t == NT - LATE - 1:
                 tables_write()
-            if t % 2 == 1 and t >= 3:
+            if t in (5, 7):
                 w_quant(t // 2 - 1)
                 x_quant(t // 2 - 1)
             if t in (5, 6):
                 products(issued)
                 products(issued + 1)
                 issued += 2
-        tables_turn(TK)
+        for k in (0, 1):
+            tables_turn(k)
 
         grouped = NT - LATE
         for i in range(NQ * NT):
-            if i < LATE:
-                w_group(grouped)
-                load_w(grouped + 8)
-                grouped += 1
-            elif i % 2 == 0 and grouped < NC:
+            m, j = divmod(i, 2)
+            if i < LATE or (j == 0 and grouped < NC):
                 w_group(grouped)
                 grouped += 1
             if i == 2:
                 x_quant(3)
-            elif i in WQ:
-                w_quant(WQ[i])
+            elif i in W_AT:
+                w_quant(W_AT[i])
+            if j == 0 and m - 1 in TURNED:
+                turn_back(m - 1)
             while issued < NQ * NT and issued <= i + AHEAD:
                 products(issued)
                 issued += 1
             rotate(i)
-            if i % 2 == TB and i // 2 - 1 in TURNED:
-                turn_back(i // 2 - 1)
-            if i >= VTILES + VLAG:
-                finish_tile(i - VLAG)
-            elif i % 2 == 1 and i < VTILES:
-                finish(i // 2)
-        for i in range(NQ * NT - VLAG, NQ * NT):
+            if j == 1 and m not in TURNED and i < NQ * NT - 1:
+                finish(m)
+        for i in range(NQ * NT - 2, NQ * NT):
             finish_tile(i)

@@ -82,16 +82,12 @@ def tile_multiheadselfattention_pa_kernel(tc, x_bytes, x_scale, w_aq, w_ak, out_
 
         load_x(0)
         load_x(1)
-        load_w(0)
-        load_w(1)
-        load_x(2)
         nc.sync.dma_start(out=sc[:], in_=x_scale.rearrange("a b k -> (a b k)").partition_broadcast(P))
-        load_x(3)
-        load_w(2)
-        load_w(3)
-        for t in range(4, NT):
+        for t in range(2, NT):
+            load_w(t - 2)
             load_x(t)
-            load_w(t)
+        load_w(6)
+        load_w(7)
 
         zero = tmp.tile([P, 1], F32, name="zero")
         warm = tmp.tile([P, 1], F32, name="warm")
@@ -160,15 +156,12 @@ def tile_multiheadselfattention_pa_kernel(tc, x_bytes, x_scale, w_aq, w_ak, out_
             nc.vector.tensor_tensor(out=xb[:], in0=xby[:, t * KDIM:(t + 1) * KDIM].bitcast(FP8), in1=sc[:], op=ALU.mult)
             xb_t[t] = xb
 
-        def x_cast(t, vector_from=NG):
+        def x_cast(t):
             xb = xbp.tile([P, KDIM], BF16, name="xb")
             for g in range(NG):
                 out = xb[:, g * 512:(g + 1) * 512]
                 codes = xby[:, t * KDIM + g * 512:t * KDIM + (g + 1) * 512].bitcast(FP8)
-                if g >= vector_from:
-                    nc.vector.tensor_copy(out=out, in_=codes)
-                else:
-                    nc.scalar.copy(out=out, in_=codes)
+                nc.scalar.copy(out=out, in_=codes)
             xb_t[t] = xb
 
         def x_turn(t):
@@ -294,7 +287,7 @@ def tile_multiheadselfattention_pa_kernel(tc, x_bytes, x_scale, w_aq, w_ak, out_
                 nc.scalar.copy(out=ab[:, 0, j].rearrange("p h d -> p (h d)"), in_=banks[j][:])
             store(m)
 
-        def finish_tile(i):
+        def finish_tile(i, eng):
             m, j = divmod(i, 2)
             q, k = divmod(m, NK)
             ab = ab_t[m]
@@ -302,7 +295,7 @@ def tile_multiheadselfattention_pa_kernel(tc, x_bytes, x_scale, w_aq, w_ak, out_
             dst = outs[q // 2][t * P:(t + 1) * P, (q % 2) * 512:(q % 2 + 1) * 512]
             a0 = ab[:, 0, j].rearrange("p h (f i) -> p h f i", f=2)
             a1 = ab[:, 1, j].rearrange("p h (f i) -> p h f i", f=2)[:, :, ::-1, :]
-            nc.vector.tensor_tensor(out=a0, in0=a0, in1=a1, op=ALU.add)
+            eng.tensor_tensor(out=a0, in0=a0, in1=a1, op=ALU.add)
             nc.sync.dma_start(out=dst, in_=ab[:, 0, j].rearrange("p h d -> p (h d)"))
 
         def tables_turn(k):
@@ -312,35 +305,27 @@ def tile_multiheadselfattention_pa_kernel(tc, x_bytes, x_scale, w_aq, w_ak, out_
                     nc.tensor.transpose(tt[:, r, j], tab[:, 2 * k + j, r].rearrange("p f i -> p (f i)"), ident[:])
             nc.scalar.copy(out=tabt[:, k].rearrange("p r t -> p (r t)"), in_=tt[:].rearrange("p r j t -> p (r j t)"))
 
-        EARLY = 3
+        EARLY = 2
         LATE = 2
         AHEAD = 2
         issued = 0
-        x_cast(0, vector_from=2)
-        x_cast(1)
-        x_turn(0)
-        x_scale_out(0)
-        w_group(0)
-        x_turn(1)
-        x_scale_out(1)
-        w_group(1)
-        x_cast(2)
+        for t in range(EARLY):
+            x_cast(t)
         tables_sines()
-        w_quant(0)
-        x_turn(2)
-        x_scale_out(2)
         swap_write()
-        for t in range(EARLY, NT):
-            x_product(t)
+        for t in range(NT):
+            if t >= EARLY:
+                x_product(t)
             x_turn(t)
-            if t - 1 < NT - LATE:
-                w_group(t - 1)
-            x_copy(t)
-            if t == EARLY:
-                x_quant(0)
+            if t >= EARLY:
+                x_copy(t)
+            else:
+                x_scale_out(t)
+            if t < NT - LATE:
+                w_group(t)
             if t == NT - LATE - 1:
                 tables_write()
-            if t in (5, 7):
+            if t % 2 == 1 and t >= 3:
                 w_quant(t // 2 - 1)
                 x_quant(t // 2 - 1)
             if t in (5, 6):
@@ -366,7 +351,9 @@ def tile_multiheadselfattention_pa_kernel(tc, x_bytes, x_scale, w_aq, w_ak, out_
                 products(issued)
                 issued += 1
             rotate(i)
-            if j == 1 and m not in TURNED and i < NQ * NT - 1:
+            if i in (NQ * NT - 4, NQ * NT - 3):
+                finish_tile(i, nc.gpsimd)
+            elif j == 1 and m not in TURNED and i < NQ * NT - 4:
                 finish(m)
         for i in range(NQ * NT - 2, NQ * NT):
-            finish_tile(i)
+            finish_tile(i, nc.vector)

@@ -37,8 +37,8 @@ def tile_multiheadselfattention_pa_kernel(tc, x_bytes, x_scale, w_aq, w_ak, out_
     outs = [out_0.rearrange("b t h d -> (b t) (h d)"), out_1.rearrange("b t h d -> (b t) (h d)")]
     ws_in = [w_aq, w_ak]
 
-    TURNED = (1, 4, 9, 13)
-    W_AT = {5: 3, 11: 4, 12: 5, 21: 6, 22: 7}
+    TURNED = (1, 5, 9)
+    W_AT = {6: 3, 13: 4, 14: 5, 21: 6, 22: 7}
 
     with ExitStack() as ctx:
         keep = ctx.enter_context(tc.tile_pool(name="keep", bufs=1))
@@ -48,6 +48,7 @@ def tile_multiheadselfattention_pa_kernel(tc, x_bytes, x_scale, w_aq, w_ak, out_
         xgp = ctx.enter_context(tc.tile_pool(name="xgp", bufs=2))
         wgp = ctx.enter_context(tc.tile_pool(name="wgp", bufs=3))
         abp = ctx.enter_context(tc.tile_pool(name="abp", bufs=5))
+        otp = ctx.enter_context(tc.tile_pool(name="otp", bufs=2))
         psum = ctx.enter_context(tc.psum_pool(name="psum", bufs=8))
         ctx.enter_context(tc.manual_schedule())
 
@@ -57,7 +58,7 @@ def tile_multiheadselfattention_pa_kernel(tc, x_bytes, x_scale, w_aq, w_ak, out_
         ident = keep.tile([P, P], F32, name="ident")
         swap = keep.tile([P, P], F32, name="swap")
         tab = keep.tile([P, NT, 2, 2, HALF], F32, name="tab")
-        tabt = keep.tile([P, 2, 2, 2 * P], F32, name="tabt")
+        tabt_t = {}
         xc = keep.tile([P, NT * NG * P], U32, name="xc", align_bytes=64)
         xs = keep.tile([P, NT * NG * P], U8, name="xs", align_bytes=64)
         wc = keep.tile([P, NC * 512], U32, name="wc", align_bytes=64)
@@ -249,7 +250,7 @@ def tile_multiheadselfattention_pa_kernel(tc, x_bytes, x_scale, w_aq, w_ak, out_
                 nc.vector.tensor_tensor(
                     out=ab[:, :, j].rearrange("p r (h b) d -> p r h (b d)", h=2),
                     in0=ps_t[i][:].rearrange("p (h t) -> p h t", h=2).unsqueeze(1).to_broadcast([P, 2, 2, 2 * P]),
-                    in1=tabt[:, k].unsqueeze(2).to_broadcast([P, 2, 2, 2 * P]),
+                    in1=tabt_t[k][:].unsqueeze(2).to_broadcast([P, 2, 2, 2 * P]),
                     op=ALU.mult,
                 )
                 return
@@ -274,40 +275,42 @@ def tile_multiheadselfattention_pa_kernel(tc, x_bytes, x_scale, w_aq, w_ak, out_
 
         def turn_back(m):
             ab = ab_t[m]
-            banks = []
             for j in range(2):
                 res = psum.tile([P, 512], F32, name="res", tag="bank")
-                banks.append(res)
                 for h in range(4):
                     out = res[:, h * HD:(h + 1) * HD]
                     block = (h % 2) * 2 + j
                     nc.tensor.matmul(out=out, lhsT=ab[:, 0, h // 2, block], rhs=ident[:], start=True, stop=False, is_transpose=True)
                     nc.tensor.matmul(out=out, lhsT=ab[:, 1, h // 2, block], rhs=swap[:], start=False, stop=True, is_transpose=True)
-            for j in range(2):
-                nc.scalar.copy(out=ab[:, 0, j].rearrange("p h d -> p (h d)"), in_=banks[j][:])
-            store(m)
+                ot = otp.tile([P, 512], F32, name="ot")
+                nc.scalar.copy(out=ot[:], in_=res[:])
+                store_tile(2 * m + j, ot[:])
+
+        def store_tile(i, src):
+            q, t = divmod(i, NT)
+            nc.sync.dma_start(out=outs[q // 2][t * P:(t + 1) * P, (q % 2) * 512:(q % 2 + 1) * 512], in_=src)
 
         def finish_tile(i, eng):
             m, j = divmod(i, 2)
-            q, k = divmod(m, NK)
             ab = ab_t[m]
-            t = 2 * k + j
-            dst = outs[q // 2][t * P:(t + 1) * P, (q % 2) * 512:(q % 2 + 1) * 512]
             a0 = ab[:, 0, j].rearrange("p h (f i) -> p h f i", f=2)
             a1 = ab[:, 1, j].rearrange("p h (f i) -> p h f i", f=2)[:, :, ::-1, :]
             eng.tensor_tensor(out=a0, in0=a0, in1=a1, op=ALU.add)
-            nc.sync.dma_start(out=dst, in_=ab[:, 0, j].rearrange("p h d -> p (h d)"))
+            store_tile(i, ab[:, 0, j].rearrange("p h d -> p (h d)"))
 
         def tables_turn(k):
             tt = psum.tile([P, 2, 2, P], F32, name="tt", tag="bank")
             for r in range(2):
                 for j in range(2):
                     nc.tensor.transpose(tt[:, r, j], tab[:, 2 * k + j, r].rearrange("p f i -> p (f i)"), ident[:])
-            nc.scalar.copy(out=tabt[:, k].rearrange("p r t -> p (r t)"), in_=tt[:].rearrange("p r j t -> p (r j t)"))
+            tabt = keep.tile([P, 2, 2 * P], F32, name=f"tabt{k}")
+            tabt_t[k] = tabt
+            nc.scalar.copy(out=tabt[:].rearrange("p r t -> p (r t)"), in_=tt[:].rearrange("p r j t -> p (r j t)"))
 
         EARLY = 2
         LATE = 2
         AHEAD = 2
+        VFIRST = 29
         issued = 0
         for t in range(EARLY):
             x_cast(t)
@@ -332,7 +335,7 @@ def tile_multiheadselfattention_pa_kernel(tc, x_bytes, x_scale, w_aq, w_ak, out_
                 products(issued)
                 products(issued + 1)
                 issued += 2
-        for k in (0, 1):
+        for k in sorted({m % NK for m in TURNED}):
             tables_turn(k)
 
         grouped = NT - LATE
@@ -345,15 +348,15 @@ def tile_multiheadselfattention_pa_kernel(tc, x_bytes, x_scale, w_aq, w_ak, out_
                 x_quant(3)
             elif i in W_AT:
                 w_quant(W_AT[i])
-            if j == 0 and m - 1 in TURNED:
-                turn_back(m - 1)
+            if j == 0 and m - 2 in TURNED:
+                turn_back(m - 2)
             while issued < NQ * NT and issued <= i + AHEAD:
                 products(issued)
                 issued += 1
             rotate(i)
-            if i in (NQ * NT - 4, NQ * NT - 3):
+            if i == VFIRST - 1:
                 finish_tile(i, nc.gpsimd)
-            elif j == 1 and m not in TURNED and i < NQ * NT - 4:
+            elif j == 1 and m not in TURNED and i < VFIRST:
                 finish(m)
-        for i in range(NQ * NT - 2, NQ * NT):
+        for i in range(VFIRST, NQ * NT):
             finish_tile(i, nc.vector)

@@ -85,8 +85,8 @@ def tile_multiheadselfattention_pa_kernel(tc, x_bytes, x_scale, w_aq, w_ak, out_
         load_x(1)
         nc.sync.dma_start(out=sc[:], in_=x_scale.rearrange("a b k -> (a b k)").partition_broadcast(P))
         for t in range(2, NT):
-            load_w(t - 2)
             load_x(t)
+            load_w(t - 2)
         load_w(6)
         load_w(7)
 
@@ -124,10 +124,9 @@ def tile_multiheadselfattention_pa_kernel(tc, x_bytes, x_scale, w_aq, w_ak, out_
                                     op=ALU.mult)
         for hs in halves:
             nc.vector.tensor_scalar(out=ni[:, hs], in0=ang[:, hs], scalar1=1.0 / TWO_PI, scalar2=None, op0=ALU.mult)
-        for hs in halves:
-            nc.vector.tensor_copy(out=nf[:, hs], in_=ni[:, hs])
-        for hs in halves:
-            nc.vector.scalar_tensor_tensor(out=ang[:, hs], in0=nf[:, hs], scalar=-TWO_PI, in1=ang[:, hs], op0=ALU.mult, op1=ALU.add)
+        def tables_reduce():
+            nc.scalar.activation(out=nf[:], in_=ni[:].bitcast(U32), func=ACT.Copy, scale=-TWO_PI)
+            nc.gpsimd.tensor_tensor(out=ang[:], in0=nf[:], in1=ang[:], op=ALU.add)
 
         def tables_sines():
             nc.scalar.activation(out=sh[:].rearrange("p t i -> p (t i)"), in_=ang[:], func=ACT.Sin, scale=0.5)
@@ -312,8 +311,9 @@ def tile_multiheadselfattention_pa_kernel(tc, x_bytes, x_scale, w_aq, w_ak, out_
         AHEAD = 2
         VFIRST = 29
         issued = 0
-        for t in range(EARLY):
-            x_cast(t)
+        x_cast(0)
+        tables_reduce()
+        x_cast(1)
         tables_sines()
         swap_write()
         for t in range(NT):
@@ -329,8 +329,8 @@ def tile_multiheadselfattention_pa_kernel(tc, x_bytes, x_scale, w_aq, w_ak, out_
             if t == NT - LATE - 1:
                 tables_write()
             if t % 2 == 1 and t >= 3:
-                w_quant(t // 2 - 1)
                 x_quant(t // 2 - 1)
+                w_quant(t // 2 - 1)
             if t in (5, 6):
                 products(issued)
                 products(issued + 1)

from contextlib import ExitStack

import concourse.mybir as mybir
from concourse.masks import make_identity

F32 = mybir.dt.float32
BF16 = mybir.dt.bfloat16
I32 = mybir.dt.int32
U32 = mybir.dt.uint32
U8 = mybir.dt.uint8
FP8 = mybir.dt.float8_e4m3fn
FP8X4 = mybir.dt.float8_e4m3fn_x4
ALU = mybir.AluOpType
ACT = mybir.ActivationFunctionType

P = 128
TOK = 1024
KDIM = 2048
HEADS = 8
HD = 128
HALF = 64
NT = TOK // P
NK = NT // 2
NG = KDIM // 512
NQ = 4
NC = NQ * NG
FLOPS = 2 * TOK * KDIM * 2 * HEADS * HD

PI = 3.141592653589793
TWO_PI = 2.0 * PI
ROTARY_BASE = 10000.0


def tile_multiheadselfattention_pa_kernel(tc, x_bytes, x_scale, w_aq, w_ak, out_0, out_1):
    nc = tc.nc
    xrows = x_bytes.flatten_outer_dims()
    outs = [out_0.rearrange("b t h d -> (b t) (h d)"), out_1.rearrange("b t h d -> (b t) (h d)")]
    ws_in = [w_aq, w_ak]

    TURNED = (1, 5, 9)
    W_AT = {6: 3, 13: 4, 14: 5, 21: 6, 22: 7}

    with ExitStack() as ctx:
        keep = ctx.enter_context(tc.tile_pool(name="keep", bufs=1))
        tmp = ctx.enter_context(tc.tile_pool(name="tmp", bufs=1))
        wrp = ctx.enter_context(tc.tile_pool(name="wrp", bufs=8))
        xbp = ctx.enter_context(tc.tile_pool(name="xbp", bufs=3))
        xgp = ctx.enter_context(tc.tile_pool(name="xgp", bufs=2))
        wgp = ctx.enter_context(tc.tile_pool(name="wgp", bufs=3))
        abp = ctx.enter_context(tc.tile_pool(name="abp", bufs=5))
        otp = ctx.enter_context(tc.tile_pool(name="otp", bufs=2))
        psum = ctx.enter_context(tc.psum_pool(name="psum", bufs=8))
        ctx.enter_context(tc.manual_schedule())

        sc = keep.tile([P, KDIM], F32, name="sc")
        sct = keep.tile([P, NG, 4], F32, name="sct")
        xby = keep.tile([P, NT * KDIM], U8, name="xby")
        ident = keep.tile([P, P], F32, name="ident")
        swap = keep.tile([P, P], F32, name="swap")
        tab = keep.tile([P, NT, 2, 2, HALF], F32, name="tab")
        tabt_t = {}
        xc = keep.tile([P, NT * NG * P], U32, name="xc", align_bytes=64)
        xs = keep.tile([P, NT * NG * P], U8, name="xs", align_bytes=64)
        wc = keep.tile([P, NC * 512], U32, name="wc", align_bytes=64)
        wsc = keep.tile([P, NC * 512], U8, name="wsc", align_bytes=64)
        wraw_t = {}

        nc.scalar.dma_start(out=sct[:], in_=x_scale.rearrange("a b (g p s) -> p (a b g) s", p=P, s=4))

        def load_x(t):
            nc.sync.dma_start(out=xby[:, t * KDIM:(t + 1) * KDIM], in_=xrows[t * P:(t + 1) * P, :])

        def load_w(c):
            q, g = divmod(c, NG)
            w = ws_in[q // 2]
            h0 = 4 * (q % 2)
            wraw = wrp.tile([P, 4, 512], BF16, name="wraw")
            wraw_t[c] = wraw
            nc.sync.dma_start(
                out=wraw[:],
                in_=w[h0:h0 + 4, g * 512:(g + 1) * 512, :].rearrange("h (p j) d -> p h (j d)", j=4),
            )

        load_x(0)
        load_x(1)
        nc.sync.dma_start(out=sc[:], in_=x_scale.rearrange("a b k -> (a b k)").partition_broadcast(P))
        for t in range(2, NT):
            load_x(t)
            load_w(t - 2)
        load_w(6)
        load_w(7)

        zero = tmp.tile([P, 1], F32, name="zero")
        warm = tmp.tile([P, 1], F32, name="warm")
        nc.vector.memset(zero[:], 0.0)
        nc.scalar.activation(out=warm[:], in_=zero[:], func=ACT.Sin)

        ang = tmp.tile([P, NT * HALF], F32, name="ang")
        pos = tmp.tile([P, NT], F32, name="pos")
        fparts = tmp.tile([P, 2, 8], F32, name="fparts")
        freq = tmp.tile([P, 8, 8], F32, name="freq")
        ni = tmp.tile([P, NT * HALF], I32, name="ni")
        nf = tmp.tile([P, NT * HALF], F32, name="nf")
        sh = tmp.tile([P, NT, HALF], F32, name="sh")
        ch = tmp.tile([P, NT, HALF], F32, name="ch")
        sq = tmp.tile([P, NT, HALF], F32, name="sq")
        sq2 = tmp.tile([P, NT, HALF], F32, name="sq2")
        nc.gpsimd.iota(pos[:], pattern=[[P, NT]], base=0, channel_multiplier=1, allow_small_or_imprecise_dtypes=True)
        make_identity(nc, ident[:])
        W2 = NT * HALF // 2
        halves = [slice(0, W2), slice(W2, 2 * W2)]
        nc.vector.memset(fparts[:], 1.0)
        for b in range(3):
            low = 1 << b
            for part, step in ((0, 1), (1, 8)):
                v = fparts[:, part].rearrange("p (a two l) -> p a two l", two=2, l=low)[:, :, 1, :]
                nc.vector.tensor_scalar(out=v, in0=v, scalar1=ROTARY_BASE ** (-low * step / 64.0), scalar2=None, op0=ALU.mult)
        nc.vector.tensor_tensor(out=freq[:], in0=fparts[:, 1].unsqueeze(2).to_broadcast([P, 8, 8]),
                                in1=fparts[:, 0].unsqueeze(1).to_broadcast([P, 8, 8]), op=ALU.mult)
        for c, hs in enumerate(halves):
            nc.vector.tensor_tensor(out=ang[:, hs].rearrange("p (t i) -> p t i", i=HALF),
                                    in0=pos[:, c * NT // 2:(c + 1) * NT // 2].unsqueeze(2).to_broadcast([P, NT // 2, HALF]),
                                    in1=freq[:].rearrange("p a b -> p (a b)").unsqueeze(1).to_broadcast([P, NT // 2, HALF]),
                                    op=ALU.mult)
        for hs in halves:
            nc.vector.tensor_scalar(out=ni[:, hs], in0=ang[:, hs], scalar1=1.0 / TWO_PI, scalar2=None, op0=ALU.mult)
        def tables_reduce():
            nc.scalar.activation(out=nf[:], in_=ni[:].bitcast(U32), func=ACT.Copy, scale=-TWO_PI)
            nc.gpsimd.tensor_tensor(out=ang[:], in0=nf[:], in1=ang[:], op=ALU.add)

        def tables_sines():
            nc.scalar.activation(out=sh[:].rearrange("p t i -> p (t i)"), in_=ang[:], func=ACT.Sin, scale=0.5)
            nc.scalar.activation(out=ch[:].rearrange("p t i -> p (t i)"), in_=ang[:], func=ACT.Sin, scale=0.5, bias=-0.25 * PI)
            nc.scalar.activation(out=sq[:], in_=sh[:], func=ACT.Square)
            nc.scalar.activation(out=sq2[:], in_=ch[:], func=ACT.Square)

        def tables_write():
            nc.scalar.activation(out=tab[:, :, 1, 0, :], in_=sq2[:], func=ACT.Copy, scale=-2.0, bias=1.0)
            nc.scalar.activation(out=tab[:, :, 1, 1, :], in_=sq2[:], func=ACT.Copy, scale=2.0, bias=-1.0)
            nc.scalar.activation(out=tab[:, :, 0, :, :], in_=sq[:].unsqueeze(2).to_broadcast([P, NT, 2, HALF]),
                                 func=ACT.Copy, scale=-2.0, bias=1.0)

        def swap_write():
            nc.scalar.copy(out=swap[:, 0:HALF], in_=ident[:, HALF:P])
            nc.scalar.copy(out=swap[:, HALF:P], in_=ident[:, 0:HALF])

        xb_t = {}
        xg_t = {}
        xt_t = {}
        ps_t = {}
        ab_t = {}
        wg_t = {}

        def x_product(t):
            xb = xbp.tile([P, KDIM], BF16, name="xb")
            nc.vector.tensor_tensor(out=xb[:], in0=xby[:, t * KDIM:(t + 1) * KDIM].bitcast(FP8), in1=sc[:], op=ALU.mult)
            xb_t[t] = xb

        def x_cast(t):
            xb = xbp.tile([P, KDIM], BF16, name="xb")
            for g in range(NG):
                out = xb[:, g * 512:(g + 1) * 512]
                codes = xby[:, t * KDIM + g * 512:t * KDIM + (g + 1) * 512].bitcast(FP8)
                nc.scalar.copy(out=out, in_=codes)
            xb_t[t] = xb

        def x_turn(t):
            words = xb_t[t][:].bitcast(F32)
            banks = []
            for b in range(2):
                xt = psum.tile([P, 512], F32, name="xt", tag="bank")
                banks.append(xt)
                for gl in range(2):
                    g = 2 * b + gl
                    for u in range(2):
                        nc.tensor.transpose(xt[:, (2 * gl + u) * P:(2 * gl + u + 1) * P],
                                            words[:, 256 * g + u:256 * (g + 1):2], ident[:])
            xt_t[t] = banks

        def x_pair_tile(t):
            if t % 2 == 0:
                xg = xgp.tile([P, 2 * KDIM], BF16, name="xg", align_bytes=64)
                xg_t[t // 2] = xg
            return xg_t[t // 2]

        def x_scale_out(t):
            dst = x_pair_tile(t)[:].rearrange("p (g j r u e) -> p g j r u e", g=NG, j=2, u=2, e=2)[:, :, t % 2]
            for g in range(NG):
                bank = xt_t[t][g // 2][:].bitcast(BF16).rearrange("p (g u r e) -> p g r u e", g=2, u=2, e=2)
                nc.vector.tensor_tensor(out=dst[:, g], in0=bank[:, g % 2],
                                        in1=sct[:, g].rearrange("p (u e) -> p u e", u=2).unsqueeze(1).to_broadcast([P, P, 2, 2]),
                                        op=ALU.mult)

        def x_copy(t):
            dst = x_pair_tile(t)[:].bitcast(F32).rearrange("p (g j r u) -> p g j r u", g=NG, j=2, u=2)[:, :, t % 2]
            for b in range(2):
                nc.scalar.copy(out=dst[:, 2 * b:2 * b + 2], in_=xt_t[t][b][:].rearrange("p (g u r) -> p g r u", g=2, u=2))

        def x_quant(k):
            lo = k * 2 * NG * P
            hi = lo + 2 * NG * P
            nc.vector.quantize_mx(out=xc[:, lo:hi].bitcast(FP8X4), scales=xs[:, lo:hi], in_=xg_t[k][:])

        def w_group(c):
            if c % 2 == 0:
                wg = wgp.tile([P, 2, 512, 4], BF16, name="wg", align_bytes=64)
                wg_t[c // 2] = wg
            wg = wg_t[c // 2]
            nc.scalar.copy(out=wg[:, c % 2].rearrange("p (h c i) j -> p h c j i", h=4, i=8),
                           in_=wraw_t[c][:].rearrange("p h (j c i) -> p h c j i", j=4, i=8))
            if c + 8 < NC:
                load_w(c + 8)

        def w_quant(k):
            lo = k * 1024
            nc.vector.quantize_mx(out=wc[:, lo:lo + 1024].bitcast(FP8X4), scales=wsc[:, lo:lo + 1024],
                                  in_=wg_t[k][:].rearrange("p e c j -> p (e c j)"))

        def products(i):
            m, j = divmod(i, 2)
            q, k = divmod(m, NK)
            ps = psum.tile([P, 512], F32, name="ps", tag="bank")
            ps_t[i] = ps
            if m in TURNED:
                for h in range(2):
                    for g in range(NG):
                        xo = (k * NG + g) * 2 * P
                        wo = (q * NG + g) * 512 + (2 * j + h) * HD
                        nc.tensor.matmul_mx(out=ps[:, h * 2 * P:(h + 1) * 2 * P],
                                            lhsT=wc[:, wo:wo + HD].bitcast(FP8X4), lhsT_scale=wsc[:, wo:wo + HD],
                                            rhs=xc[:, xo:xo + 2 * P].bitcast(FP8X4), rhs_scale=xs[:, xo:xo + 2 * P],
                                            start=(g == 0), stop=(g == NG - 1))
                return
            for g in range(NG):
                xo = (k * NG + g) * 2 * P + j * P
                wo = (q * NG + g) * 512
                nc.tensor.matmul_mx(out=ps[:], lhsT=xc[:, xo:xo + P].bitcast(FP8X4), lhsT_scale=xs[:, xo:xo + P],
                                    rhs=wc[:, wo:wo + 512].bitcast(FP8X4), rhs_scale=wsc[:, wo:wo + 512],
                                    start=(g == 0), stop=(g == NG - 1))

        def rotate(i):
            m, j = divmod(i, 2)
            k = m % NK
            if j == 0:
                ab = abp.tile([P, 2, 2, 4, HD], F32, name="ab")
                ab_t[m] = ab
            ab = ab_t[m]
            if m in TURNED:
                nc.vector.tensor_tensor(
                    out=ab[:, :, j].rearrange("p r (h b) d -> p r h (b d)", h=2),
                    in0=ps_t[i][:].rearrange("p (h t) -> p h t", h=2).unsqueeze(1).to_broadcast([P, 2, 2, 2 * P]),
                    in1=tabt_t[k][:].unsqueeze(2).to_broadcast([P, 2, 2, 2 * P]),
                    op=ALU.mult,
                )
                return
            nc.vector.tensor_tensor(
                out=ab[:, :, j],
                in0=ps_t[i][:].rearrange("p (h d) -> p h d", h=4).unsqueeze(1).to_broadcast([P, 2, 4, HD]),
                in1=tab[:, 2 * k + j].rearrange("p r f i -> p r (f i)").unsqueeze(2).to_broadcast([P, 2, 4, HD]),
                op=ALU.mult,
            )

        def store(m):
            q, k = divmod(m, NK)
            dst = outs[q // 2][2 * k * P:(2 * k + 2) * P, (q % 2) * 512:(q % 2 + 1) * 512].rearrange("(j p) c -> p j c", p=P)
            nc.sync.dma_start(out=dst, in_=ab_t[m][:, 0].rearrange("p j h d -> p j (h d)"))

        def finish(m):
            ab = ab_t[m]
            a0 = ab[:, 0].rearrange("p j h (f i) -> p (j h) f i", f=2)
            a1 = ab[:, 1].rearrange("p j h (f i) -> p (j h) f i", f=2)[:, :, ::-1, :]
            nc.gpsimd.tensor_tensor(out=a0, in0=a0, in1=a1, op=ALU.add)
            store(m)

        def turn_back(m):
            ab = ab_t[m]
            for j in range(2):
                res = psum.tile([P, 512], F32, name="res", tag="bank")
                for h in range(4):
                    out = res[:, h * HD:(h + 1) * HD]
                    block = (h % 2) * 2 + j
                    nc.tensor.matmul(out=out, lhsT=ab[:, 0, h // 2, block], rhs=ident[:], start=True, stop=False, is_transpose=True)
                    nc.tensor.matmul(out=out, lhsT=ab[:, 1, h // 2, block], rhs=swap[:], start=False, stop=True, is_transpose=True)
                ot = otp.tile([P, 512], F32, name="ot")
                nc.scalar.copy(out=ot[:], in_=res[:])
                store_tile(2 * m + j, ot[:])

        def store_tile(i, src):
            q, t = divmod(i, NT)
            nc.sync.dma_start(out=outs[q // 2][t * P:(t + 1) * P, (q % 2) * 512:(q % 2 + 1) * 512], in_=src)

        def finish_tile(i, eng):
            m, j = divmod(i, 2)
            ab = ab_t[m]
            a0 = ab[:, 0, j].rearrange("p h (f i) -> p h f i", f=2)
            a1 = ab[:, 1, j].rearrange("p h (f i) -> p h f i", f=2)[:, :, ::-1, :]
            eng.tensor_tensor(out=a0, in0=a0, in1=a1, op=ALU.add)
            store_tile(i, ab[:, 0, j].rearrange("p h d -> p (h d)"))

        def tables_turn(k):
            tt = psum.tile([P, 2, 2, P], F32, name="tt", tag="bank")
            for r in range(2):
                for j in range(2):
                    nc.tensor.transpose(tt[:, r, j], tab[:, 2 * k + j, r].rearrange("p f i -> p (f i)"), ident[:])
            tabt = keep.tile([P, 2, 2 * P], F32, name=f"tabt{k}")
            tabt_t[k] = tabt
            nc.scalar.copy(out=tabt[:].rearrange("p r t -> p (r t)"), in_=tt[:].rearrange("p r j t -> p (r j t)"))

        EARLY = 2
        LATE = 2
        AHEAD = 2
        VFIRST = 29
        issued = 0
        x_cast(0)
        tables_reduce()
        x_cast(1)
        tables_sines()
        swap_write()
        for t in range(NT):
            if t >= EARLY:
                x_product(t)
            x_turn(t)
            if t >= EARLY:
                x_copy(t)
            else:
                x_scale_out(t)
            if t < NT - LATE:
                w_group(t)
            if t == NT - LATE - 1:
                tables_write()
            if t % 2 == 1 and t >= 3:
                x_quant(t // 2 - 1)
                w_quant(t // 2 - 1)
            if t in (5, 6):
                products(issued)
                products(issued + 1)
                issued += 2
        for k in sorted({m % NK for m in TURNED}):
            tables_turn(k)

        grouped = NT - LATE
        for i in range(NQ * NT):
            m, j = divmod(i, 2)
            if i < LATE or (j == 0 and grouped < NC):
                w_group(grouped)
                grouped += 1
            if i == 2:
                x_quant(3)
            elif i in W_AT:
                w_quant(W_AT[i])
            if j == 0 and m - 2 in TURNED:
                turn_back(m - 2)
            while issued < NQ * NT and issued <= i + AHEAD:
                products(issued)
                issued += 1
            rotate(i)
            if i == VFIRST - 1:
                finish_tile(i, nc.gpsimd)
            elif j == 1 and m not in TURNED and i < VFIRST:
                finish(m)
        for i in range(VFIRST, NQ * NT):
            finish_tile(i, nc.vector)
